import numpy as np
import ml_dtypes


def mxq(x, axis, fmt="e4m3"):
    dtype, down = {"e4m3": (ml_dtypes.float8_e4m3fn, 7), "e5m2": (ml_dtypes.float8_e5m2, 14)}[fmt]
    v = np.moveaxis(np.asarray(x, np.float32).astype(ml_dtypes.bfloat16).astype(np.float64), axis, -1)
    blocks = v.reshape(v.shape[:-1] + (-1, 32))
    amax = np.abs(blocks).max(-1, keepdims=True)
    byte = np.maximum(np.where(amax > 0, np.frexp(amax)[1] - 1 + 127, 0) - down, 1)
    scale = np.exp2(byte - 127.0)
    codes = (blocks / scale).astype(np.float32).astype(dtype).astype(np.float64)
    return np.moveaxis((codes * scale).reshape(v.shape), -1, axis)


WIDE = False


def mx_kscale(k):
    if not WIDE:
        return np.ones(k)
    levels = np.array([10, -10, 5, -5, 0])
    a = np.random.permutation(np.resize(levels, k // 512 * 4)).reshape(k // 512, 4)
    idx = np.arange(k)
    return np.exp2(a[idx // 512, idx % 128 // 32])


BF16 = ml_dtypes.bfloat16


def bf(x):
    return np.asarray(x, np.float32).astype(BF16)


def f64(x):
    return np.asarray(x).astype(np.float64)


B, N1, N2, D, H, DH = 4, 384, 128, 1024, 8, 128
E = H * DH


def rope_tables(n, d):
    inv = 1.0 / (10000.0 ** (np.arange(0, d, 2) / d))
    ang = np.outer(np.arange(n), inv)
    return np.repeat(np.cos(ang), 2, axis=-1), np.repeat(np.sin(ang), 2, axis=-1)


def apply_rope(x, cos, sin):
    xr = x.reshape(x.shape[:-1] + (-1, 2))
    x_real, x_imag = xr[..., 0], xr[..., 1]
    x_rot = np.stack([-x_imag, x_real], axis=-1).reshape(x.shape)
    return x * cos[None, None] + x_rot * sin[None, None]


def split_heads(t):
    b, n, _ = t.shape
    return t.reshape(b, n, H, DH).transpose(0, 2, 1, 3)


def setup_inputs():
    s1, s2 = mx_kscale(D), mx_kscale(D)
    cos1, sin1 = rope_tables(N1, DH)
    cos2, sin2 = rope_tables(N2, DH)

    def w(s):
        return bf(np.random.standard_normal((D, E)) * 1.4 / np.sqrt(D) / s[:, None])

    def b():
        return bf(np.random.standard_normal(E) * 0.3)

    return {"x_1": bf(np.random.standard_normal((B, N1, D)) * s1), "x_2": bf(np.random.standard_normal((B, N2, D)) * s2),
            "cos1": bf(cos1), "sin1": bf(sin1), "cos2": bf(cos2), "sin2": bf(sin2),
            "wq1": w(s1), "bq1": b(), "wk1": w(s1), "bk1": b(),
            "wq2": w(s2), "bq2": b(), "wk2": w(s2), "bk2": b()}


def reference(x_1, x_2, cos1, sin1, cos2, sin2, wq1, bq1, wk1, bk1, wq2, bq2, wk2, bk2):
    x1q = mxq(f64(x_1), 2, "e4m3")
    x2q = mxq(f64(x_2), 2, "e4m3")
    q = np.concatenate([(x1q @ mxq(f64(wq1), 0, "e4m3")) + f64(bq1),
                        (x2q @ mxq(f64(wq2), 0, "e4m3")) + f64(bq2)], axis=1)
    k = np.concatenate([(x1q @ mxq(f64(wk1), 0, "e4m3")) + f64(bk1),
                        (x2q @ mxq(f64(wk2), 0, "e4m3")) + f64(bk2)], axis=1)
    q, k = split_heads(q), split_heads(k)
    q = q * (DH ** -0.5)
    cos = np.concatenate([f64(cos1), f64(cos2)], axis=0)
    sin = np.concatenate([f64(sin1), f64(sin2)], axis=0)
    return apply_rope(q, cos, sin), apply_rope(k, cos, sin)

@@ -1,0 +1,285 @@
+from contextlib import ExitStack
+
+import concourse.masks as masks
+import concourse.mybir as mybir
+
+F32 = mybir.dt.float32
+BF16 = mybir.dt.bfloat16
+U32 = mybir.dt.uint32
+U8 = mybir.dt.uint8
+FP8X4 = mybir.dt.float8_e4m3fn_x4
+MULT = mybir.AluOpType.mult
+ADD = mybir.AluOpType.add
+IDENTITY = mybir.ActivationFunctionType.Identity
+
+P = 128
+D = 1024
+HEADS = 8
+DH = 128
+N1 = 384
+Q_SCALE = DH ** -0.5
+FLOPS = 2 * 2048 * 1024 * 2048
+
+MANUAL = True
+
+SLICES = [(0, 0), (0, 1), (2, 0), (2, 1), (1, 0), (1, 1), (3, 0), (3, 1)]
+
+
+def tile_dualmultiheadattention_pa_kernel(
+    tc, x_1, x_2, cos1, sin1, cos2, sin2, wq1, bq1, wk1, bk1, wq2, bq2, wk2, bk2, out_0, out_1
+):
+    nc = tc.nc
+    weights = [wq1, wq2, wk1, wk2]
+    biases = [bq1, bq2, bk1, bk2]
+    outs = [out_0, out_0, out_1, out_1]
+
+    rounds = []
+    for sl in range(8):
+        if SLICES[sl][0] in (0, 2):
+            rounds.extend([(sl, 0), (sl, 1), (sl, 2)])
+        else:
+            rounds.append((sl, 3))
+    n_rounds = len(rounds)
+
+    with ExitStack() as ctx:
+        const = ctx.enter_context(tc.tile_pool(name="const", bufs=1))
+        raw = ctx.enter_context(tc.tile_pool(name="raw", bufs=1))
+        xgp = ctx.enter_context(tc.tile_pool(name="xgp", bufs=2))
+        wgp = ctx.enter_context(tc.tile_pool(name="wgp", bufs=2))
+        wcp = ctx.enter_context(tc.tile_pool(name="wcp", bufs=4))
+        up = ctx.enter_context(tc.tile_pool(name="up", bufs=8))
+        abp = ctx.enter_context(tc.tile_pool(name="abp", bufs=3))
+        y1p = ctx.enter_context(tc.tile_pool(name="y1p", bufs=3))
+        y2p = ctx.enter_context(tc.tile_pool(name="y2p", bufs=3))
+        ps1p = ctx.enter_context(tc.psum_pool(name="ps1p", bufs=3))
+        ps2p = ctx.enter_context(tc.psum_pool(name="ps2p", bufs=5))
+        if MANUAL:
+            ctx.enter_context(tc.manual_schedule())
+
+        ident = const.tile([P, P], F32, name="ident")
+        masks.make_identity(nc, ident[:])
+
+        x1r = [raw.tile([P, 3, D], BF16, name="x1r%d" % b) for b in range(4)]
+        x2r = raw.tile([P, 4, D], BF16, name="x2r")
+        wraw = [raw.tile([P, 2, 4, D], BF16, name="wraw%d" % w) for w in range(4)]
+
+        def load_w(w, c0, c1):
+            src = weights[w].rearrange("(m q e) c -> q m e c", m=4, e=2)
+            dst = wraw[w][:].rearrange("q g (u e) c -> q (g u) e c", e=2)
+            for e in range(2):
+                nc.sync.dma_start(out=dst[:, :, e, c0:c1], in_=src[:, :, e, c0:c1])
+
+        def load_w_full(w):
+            nc.sync.dma_start(
+                out=wraw[w][:].rearrange("q g (u e) c -> q (g u) (e c)", e=2),
+                in_=weights[w].rearrange("(m q e) c -> q m (e c)", m=4, e=2),
+            )
+
+        load_w(0, 0, 512)
+        for b in range(4):
+            nc.sync.dma_start(out=x1r[b][:], in_=x_1[b].rearrange("(p j) k -> p j k", j=3))
+        load_w(0, 512, 1024)
+        load_w_full(2)
+        nc.sync.dma_start(out=x2r[:], in_=x_2.rearrange("b p k -> p b k"))
+        load_w_full(1)
+        load_w_full(3)
+
+        btile = const.tile([P, P], BF16, name="btile")
+        nc.vector.memset(btile[:], 0.0)
+        for w in range(4):
+            nc.scalar.dma_start(out=btile[8 * w : 8 * w + 8, :], in_=biases[w].rearrange("(h c) -> h c", c=DH))
+        ctr = const.tile([P, 4, DH], BF16, name="ctr")
+        strw = const.tile([P, 4, DH], BF16, name="strw")
+        nc.scalar.dma_start(out=ctr[:, 0:3, :], in_=cos1.rearrange("(p j) c -> p j c", j=3))
+        nc.scalar.dma_start(out=ctr[:, 3, :], in_=cos2)
+        nc.scalar.dma_start(out=strw[:, 0:3, :], in_=sin1.rearrange("(p j) c -> p j c", j=3))
+        nc.scalar.dma_start(out=strw[:, 3, :], in_=sin2)
+
+        bt32 = const.tile([P, P], F32, name="bt32")
+        nc.vector.tensor_copy(out=bt32[:], in_=btile[:])
+        pb = ps2p.tile([P, 512], F32, name="ps2", tag="ps2")
+        nc.tensor.transpose(pb[:, 0:P], bt32[:], ident[:])
+        bcol = const.tile([P, 32], F32, name="bcol")
+        nc.vector.tensor_scalar_mul(out=bcol[:, 0:16], in0=pb[:, 0:16], scalar1=Q_SCALE)
+        nc.vector.tensor_copy(out=bcol[:, 16:32], in_=pb[:, 16:32])
+
+        ctab = const.tile([P, 4, DH], F32, name="ctab")
+        nc.vector.tensor_copy(out=ctab[:], in_=ctr[:])
+        stab = const.tile([P, 4, 2, DH // 2], F32, name="stab")
+        spair = strw[:].rearrange("p s (j e) -> p s j e", e=2)
+        nc.vector.tensor_scalar_mul(out=stab[:, :, 0, :], in0=spair[:, :, :, 0], scalar1=-1.0)
+        nc.vector.tensor_copy(out=stab[:, :, 1, :], in_=spair[:, :, :, 1])
+
+        xc = [const.tile([P, 2, 512], U32, name="xc%d" % g, align_bytes=64) for g in range(4)]
+        xs = [const.tile([P, 2, 512], U8, name="xs%d" % g, align_bytes=64) for g in range(4)]
+
+        def x_transposes(grp, engines):
+            xg = xgp.tile([P, 2, 512, 4], BF16, name="xg", tag="xg", align_bytes=64)
+            xg32 = xg[:].bitcast(F32)
+            for tl in range(4):
+                tau = 4 * grp + tl
+                if tau < 12:
+                    src = x1r[tau // 3][:, tau % 3, :].bitcast(F32)
+                else:
+                    src = x2r[:, tau - 12, :].bitcast(F32)
+                xt = ps1p.tile([P, 512], F32, name="ps1", tag="ps1")
+                for m in range(4):
+                    nc.tensor.transpose(xt[:, P * m : P * m + P], src[:, P * m : P * m + P], ident[:])
+                dst = xg32[:, :, P * tl : P * tl + P, :]
+                view = xt[:].rearrange("p (g u t) -> p g t u", g=2, u=2)
+                if engines[tl] == "s":
+                    nc.scalar.copy(out=dst, in_=view)
+                else:
+                    nc.vector.tensor_copy(out=dst, in_=view)
+            return xg
+
+        def x_quantise(grp, xg):
+            for g in range(2):
+                nc.vector.quantize_mx(
+                    out=xc[grp][:, g, :].bitcast(FP8X4),
+                    scales=xs[grp][:, g, :],
+                    in_=xg[:, g, :, :].rearrange("p t k -> p (t k)"),
+                )
+
+        wg_tiles = {}
+        w_codes = {}
+
+        def w_regroup(sl, g, engine):
+            w, s = SLICES[sl]
+            if g == 0:
+                wg_tiles[sl] = wgp.tile([P, 2, 512, 4], BF16, name="wg", tag="wg", align_bytes=64)
+            src = wraw[w][:, g, :, 512 * s : 512 * s + 512].rearrange("p t (c i) -> p c t i", i=4)
+            dst = wg_tiles[sl][:, g, :, :].rearrange("p (c i) t -> p c t i", i=4)
+            if engine == "s":
+                nc.scalar.copy(out=dst, in_=src)
+            else:
+                nc.vector.tensor_copy(out=dst, in_=src)
+
+        def w_quantise(sl):
+            wc = wcp.tile([P, 2, 512], U32, name="wc", tag="wc", align_bytes=64)
+            ws = wcp.tile([P, 2, 512], U8, name="ws", tag="ws", align_bytes=64)
+            nc.vector.quantize_mx(
+                out=wc[:].rearrange("p g c -> p (g c)").bitcast(FP8X4),
+                scales=ws[:].rearrange("p g c -> p (g c)"),
+                in_=wg_tiles[sl][:].rearrange("p g c t -> p (g c t)"),
+            )
+            w_codes[sl] = (wc, ws)
+
+        u_tiles = {}
+
+        def project(r):
+            sl, grp = rounds[r]
+            w, s = SLICES[sl]
+            wc, ws = w_codes[sl]
+            scale = Q_SCALE if w < 2 else 1.0
+            us = []
+            for hh in range(4):
+                ps = ps1p.tile([P, 512], F32, name="ps1", tag="ps1")
+                for g in range(2):
+                    nc.tensor.matmul_mx(
+                        out=ps[:],
+                        lhsT=wc[:, g, P * hh : P * hh + P].bitcast(FP8X4),
+                        lhsT_scale=ws[:, g, P * hh : P * hh + P],
+                        rhs=xc[grp][:, g, :].bitcast(FP8X4),
+                        rhs_scale=xs[grp][:, g, :],
+                        start=(g == 0),
+                        stop=(g == 1),
+                    )
+                u = up.tile([P, 512], F32, name="u", tag="u")
+                col = 8 * w + 4 * s + hh
+                nc.scalar.activation(out=u[:], in_=ps[:], func=IDENTITY, bias=bcol[:, col : col + 1], scale=scale)
+                us.append(u)
+            u_tiles[r] = us
+
+        y_open = {}
+        ps2_tiles = {}
+
+        def back_transposes(r):
+            us = u_tiles[r]
+            banks = []
+            for tl in range(4):
+                ps2 = ps2p.tile([P, 512], F32, name="ps2", tag="ps2")
+                for hh in range(4):
+                    nc.tensor.transpose(ps2[:, P * hh : P * hh + P], us[hh][:, P * tl : P * tl + P], ident[:])
+                banks.append(ps2)
+            ps2_tiles[r] = banks
+
+        def rope(r, tl):
+            sl, grp = rounds[r]
+            w, s = SLICES[sl]
+            out_t = outs[w]
+            tau = 4 * grp + tl
+            ps2 = ps2_tiles[r][tl]
+            slot = tau % 3 if tau < 12 else 3
+            a = abp.tile([P, 4, DH], F32, name="a", tag="a")
+            nc.vector.tensor_tensor(
+                out=a[:],
+                in0=ps2[:].rearrange("p (h c) -> p h c", h=4),
+                in1=ctab[:, slot, :].unsqueeze(1).to_broadcast([P, 4, DH]),
+                op=MULT,
+            )
+            bt = abp.tile([P, 2, 4, DH // 2], F32, name="bt", tag="bt")
+            pairs = ps2[:].rearrange("p (h j e) -> p h j e", h=4, e=2)
+            for e in range(2):
+                nc.vector.tensor_tensor(
+                    out=bt[:, e, :, :],
+                    in0=pairs[:, :, :, 1 - e],
+                    in1=stab[:, slot, e, :].unsqueeze(1).to_broadcast([P, 4, DH // 2]),
+                    op=MULT,
+                )
+            if tau < 12:
+                b, jt = tau // 3, tau % 3
+                if jt == 0:
+                    y_open[b] = y1p.tile([P, 4, 3, DH], F32, name="y1", tag="y1")
+                y = y_open[b]
+                yv = y[:, :, jt, :]
+            else:
+                b, jt = tau - 12, 0
+                y = y2p.tile([P, 4, DH], F32, name="y2", tag="y2")
+                yv = y[:]
+            nc.gpsimd.tensor_tensor(
+                out=yv.rearrange("p h (j e) -> p h j e", e=2),
+                in0=a[:].rearrange("p h (j e) -> p h j e", e=2),
+                in1=bt[:].rearrange("p e h j -> p h j e"),
+                op=ADD,
+            )
+            if tau < 12:
+                if jt == 2:
+                    nc.sync.dma_start(
+                        out=out_t[b, 4 * s : 4 * s + 4, 0:N1, :].rearrange("h (p j) c -> p h (j c)", j=3),
+                        in_=y[:].rearrange("p h j c -> p h (j c)"),
+                    )
+            else:
+                nc.sync.dma_start(
+                    out=out_t[b, 4 * s : 4 * s + 4, N1:512, :].rearrange("h p c -> p h c"),
+                    in_=y[:],
+                )
+
+        w_regroup(0, 0, "v")
+        w_regroup(0, 1, "v")
+        w_quantise(0)
+        xg0 = x_transposes(0, "ssss")
+        x_quantise(0, xg0)
+        xg1 = x_transposes(1, "ssvv")
+        project(0)
+        x_quantise(1, xg1)
+
+        jobs = [(sl, g) for sl in range(1, 8) for g in range(2)]
+        quantise_after = {1: 1, 4: 2, 6: 3, 8: 4, 10: 5, 12: 6, 13: 7}
+        xg_late = {}
+        for i in range(n_rounds):
+            back_transposes(i)
+            if i == 0:
+                xg_late[0] = (2, x_transposes(2, "ssss"))
+            if i + 1 < n_rounds:
+                project(i + 1)
+            if i == 6:
+                xg_late[7] = (3, x_transposes(3, "ssss"))
+            if i < len(jobs):
+                w_regroup(jobs[i][0], jobs[i][1], "s")
+            for tl in range(4):
+                rope(i, tl)
+            if i in xg_late:
+                x_quantise(xg_late[i][0], xg_late[i][1])
+            if i in quantise_after:
+                w_quantise(quantise_after[i])

@@ -10,11 +10,9 @@ U8 = mybir.dt.uint8
 FP8X4 = mybir.dt.float8_e4m3fn_x4
 MULT = mybir.AluOpType.mult
 ADD = mybir.AluOpType.add
-IDENTITY = mybir.ActivationFunctionType.Identity
 
 P = 128
 D = 1024
-HEADS = 8
 DH = 128
 N1 = 384
 Q_SCALE = DH ** -0.5
@@ -47,21 +45,28 @@ def tile_dualmultiheadattention_pa_kernel(
         xgp = ctx.enter_context(tc.tile_pool(name="xgp", bufs=2))
         wgp = ctx.enter_context(tc.tile_pool(name="wgp", bufs=2))
         wcp = ctx.enter_context(tc.tile_pool(name="wcp", bufs=4))
-        up = ctx.enter_context(tc.tile_pool(name="up", bufs=8))
-        abp = ctx.enter_context(tc.tile_pool(name="abp", bufs=3))
+        abp = ctx.enter_context(tc.tile_pool(name="abp", bufs=8))
         y1p = ctx.enter_context(tc.tile_pool(name="y1p", bufs=3))
         y2p = ctx.enter_context(tc.tile_pool(name="y2p", bufs=3))
-        ps1p = ctx.enter_context(tc.psum_pool(name="ps1p", bufs=3))
-        ps2p = ctx.enter_context(tc.psum_pool(name="ps2p", bufs=5))
+        ps1p = ctx.enter_context(tc.psum_pool(name="ps1p", bufs=4))
+        ps2p = ctx.enter_context(tc.psum_pool(name="ps2p", bufs=4))
         if MANUAL:
             ctx.enter_context(tc.manual_schedule())
 
         ident = const.tile([P, P], F32, name="ident")
         masks.make_identity(nc, ident[:])
+        pswap = const.tile([P, P], F32, name="pswap")
+        for e in range(2):
+            nc.gpsimd.tensor_copy(
+                out=pswap[:].rearrange("p (j e) -> p j e", e=2)[:, :, e],
+                in_=ident[:].rearrange("p (j e) -> p j e", e=2)[:, :, 1 - e],
+            )
 
         x1r = [raw.tile([P, 3, D], BF16, name="x1r%d" % b) for b in range(4)]
         x2r = raw.tile([P, 4, D], BF16, name="x2r")
-        wraw = [raw.tile([P, 2, 4, D], BF16, name="wraw%d" % w) for w in range(4)]
+        wraw = {}
+        for w in (0, 2, 1):
+            wraw[w] = raw.tile([P, 2, 4, D], BF16, name="wraw%d" % w)
 
         def load_w(w, c0, c1):
             src = weights[w].rearrange("(m q e) c -> q m e c", m=4, e=2)
@@ -82,7 +87,6 @@ def tile_dualmultiheadattention_pa_kernel(
         load_w_full(2)
         nc.sync.dma_start(out=x2r[:], in_=x_2.rearrange("b p k -> p b k"))
         load_w_full(1)
-        load_w_full(3)
 
         btile = const.tile([P, P], BF16, name="btile")
         nc.vector.memset(btile[:], 0.0)
@@ -94,21 +98,6 @@ def tile_dualmultiheadattention_pa_kernel(
         nc.scalar.dma_start(out=ctr[:, 3, :], in_=cos2)
         nc.scalar.dma_start(out=strw[:, 0:3, :], in_=sin1.rearrange("(p j) c -> p j c", j=3))
         nc.scalar.dma_start(out=strw[:, 3, :], in_=sin2)
-
-        bt32 = const.tile([P, P], F32, name="bt32")
-        nc.vector.tensor_copy(out=bt32[:], in_=btile[:])
-        pb = ps2p.tile([P, 512], F32, name="ps2", tag="ps2")
-        nc.tensor.transpose(pb[:, 0:P], bt32[:], ident[:])
-        bcol = const.tile([P, 32], F32, name="bcol")
-        nc.vector.tensor_scalar_mul(out=bcol[:, 0:16], in0=pb[:, 0:16], scalar1=Q_SCALE)
-        nc.vector.tensor_copy(out=bcol[:, 16:32], in_=pb[:, 16:32])
-
-        ctab = const.tile([P, 4, DH], F32, name="ctab")
-        nc.vector.tensor_copy(out=ctab[:], in_=ctr[:])
-        stab = const.tile([P, 4, 2, DH // 2], F32, name="stab")
-        spair = strw[:].rearrange("p s (j e) -> p s j e", e=2)
-        nc.vector.tensor_scalar_mul(out=stab[:, :, 0, :], in0=spair[:, :, :, 0], scalar1=-1.0)
-        nc.vector.tensor_copy(out=stab[:, :, 1, :], in_=spair[:, :, :, 1])
 
         xc = [const.tile([P, 2, 512], U32, name="xc%d" % g, align_bytes=64) for g in range(4)]
         xs = [const.tile([P, 2, 512], U8, name="xs%d" % g, align_bytes=64) for g in range(4)]
@@ -122,7 +111,7 @@ def tile_dualmultiheadattention_pa_kernel(
                     src = x1r[tau // 3][:, tau % 3, :].bitcast(F32)
                 else:
                     src = x2r[:, tau - 12, :].bitcast(F32)
-                xt = ps1p.tile([P, 512], F32, name="ps1", tag="ps1")
+                xt = ps2p.tile([P, 512], F32, name="ps2", tag="ps2")
                 for m in range(4):
                     nc.tensor.transpose(xt[:, P * m : P * m + P], src[:, P * m : P * m + P], ident[:])
                 dst = xg32[:, :, P * tl : P * tl + P, :]
@@ -165,14 +154,13 @@ def tile_dualmultiheadattention_pa_kernel(
             )
             w_codes[sl] = (wc, ws)
 
-        u_tiles = {}
+        ps1_tiles = {}
+        ab_tiles = {}
 
         def project(r):
             sl, grp = rounds[r]
-            w, s = SLICES[sl]
             wc, ws = w_codes[sl]
-            scale = Q_SCALE if w < 2 else 1.0
-            us = []
+            banks = []
             for hh in range(4):
                 ps = ps1p.tile([P, 512], F32, name="ps1", tag="ps1")
                 for g in range(2):
@@ -185,101 +173,142 @@ def tile_dualmultiheadattention_pa_kernel(
                         start=(g == 0),
                         stop=(g == 1),
                     )
-                u = up.tile([P, 512], F32, name="u", tag="u")
-                col = 8 * w + 4 * s + hh
-                nc.scalar.activation(out=u[:], in_=ps[:], func=IDENTITY, bias=bcol[:, col : col + 1], scale=scale)
-                us.append(u)
-            u_tiles[r] = us
+                banks.append(ps)
+            ps1_tiles[r] = banks
+            ab_tiles[r] = []
+
+        def products(r, hh):
+            sl, grp = rounds[r]
+            w, s = SLICES[sl]
+            col = 8 * w + 4 * s + hh
+            ps = ps1_tiles[r][hh]
+            pair = []
+            for name, long_table, short_table in (("a", ct1, ct2), ("b", st1, st2)):
+                t = abp.tile([P, 512], F32, name=name, tag=name)
+                if grp < 3:
+                    nc.vector.scalar_tensor_tensor(
+                        out=t[:], in0=ps[:], scalar=bcol[:, col : col + 1],
+                        in1=long_table[:, P * grp : P * grp + 512], op0=ADD, op1=MULT,
+                    )
+                else:
+                    nc.vector.scalar_tensor_tensor(
+                        out=t[:].rearrange("p (t n) -> p t n", t=4),
+                        in0=ps[:].rearrange("p (t n) -> p t n", t=4),
+                        scalar=bcol[:, col : col + 1],
+                        in1=short_table[:].unsqueeze(1).to_broadcast([P, 4, P]),
+                        op0=ADD, op1=MULT,
+                    )
+                pair.append(t)
+            ab_tiles[r].append(pair)
 
         y_open = {}
-        ps2_tiles = {}
 
-        def back_transposes(r):
-            us = u_tiles[r]
-            banks = []
-            for tl in range(4):
-                ps2 = ps2p.tile([P, 512], F32, name="ps2", tag="ps2")
-                for hh in range(4):
-                    nc.tensor.transpose(ps2[:, P * hh : P * hh + P], us[hh][:, P * tl : P * tl + P], ident[:])
-                banks.append(ps2)
-            ps2_tiles[r] = banks
-
-        def rope(r, tl):
+        def finish(r):
             sl, grp = rounds[r]
             w, s = SLICES[sl]
             out_t = outs[w]
-            tau = 4 * grp + tl
-            ps2 = ps2_tiles[r][tl]
-            slot = tau % 3 if tau < 12 else 3
-            a = abp.tile([P, 4, DH], F32, name="a", tag="a")
-            nc.vector.tensor_tensor(
-                out=a[:],
-                in0=ps2[:].rearrange("p (h c) -> p h c", h=4),
-                in1=ctab[:, slot, :].unsqueeze(1).to_broadcast([P, 4, DH]),
-                op=MULT,
-            )
-            bt = abp.tile([P, 2, 4, DH // 2], F32, name="bt", tag="bt")
-            pairs = ps2[:].rearrange("p (h j e) -> p h j e", h=4, e=2)
-            for e in range(2):
-                nc.vector.tensor_tensor(
-                    out=bt[:, e, :, :],
-                    in0=pairs[:, :, :, 1 - e],
-                    in1=stab[:, slot, e, :].unsqueeze(1).to_broadcast([P, 4, DH // 2]),
-                    op=MULT,
-                )
-            if tau < 12:
-                b, jt = tau // 3, tau % 3
-                if jt == 0:
-                    y_open[b] = y1p.tile([P, 4, 3, DH], F32, name="y1", tag="y1")
-                y = y_open[b]
-                yv = y[:, :, jt, :]
-            else:
-                b, jt = tau - 12, 0
-                y = y2p.tile([P, 4, DH], F32, name="y2", tag="y2")
-                yv = y[:]
-            nc.gpsimd.tensor_tensor(
-                out=yv.rearrange("p h (j e) -> p h j e", e=2),
-                in0=a[:].rearrange("p h (j e) -> p h j e", e=2),
-                in1=bt[:].rearrange("p e h j -> p h j e"),
-                op=ADD,
-            )
-            if tau < 12:
-                if jt == 2:
-                    nc.sync.dma_start(
-                        out=out_t[b, 4 * s : 4 * s + 4, 0:N1, :].rearrange("h (p j) c -> p h (j c)", j=3),
-                        in_=y[:].rearrange("p h j c -> p h (j c)"),
+            for tl in range(4):
+                tau = 4 * grp + tl
+                ps2 = ps2p.tile([P, 512], F32, name="ps2", tag="ps2")
+                for hh in range(4):
+                    a, b2 = ab_tiles[r][hh]
+                    nc.tensor.matmul(
+                        out=ps2[:, P * hh : P * hh + P], lhsT=a[:, P * tl : P * tl + P], rhs=ident[:],
+                        start=True, stop=False, is_transpose=True,
                     )
-            else:
-                nc.sync.dma_start(
-                    out=out_t[b, 4 * s : 4 * s + 4, N1:512, :].rearrange("h p c -> p h c"),
-                    in_=y[:],
-                )
+                    nc.tensor.matmul(
+                        out=ps2[:, P * hh : P * hh + P], lhsT=b2[:, P * tl : P * tl + P], rhs=pswap[:],
+                        start=False, stop=True, is_transpose=True,
+                    )
+                if tau < 12:
+                    b, jt = tau // 3, tau % 3
+                    if jt == 0:
+                        y_open[b] = y1p.tile([P, 4, 3, DH], F32, name="y1", tag="y1")
+                    y = y_open[b]
+                    yv = y[:, :, jt, :]
+                else:
+                    b, jt = tau - 12, 0
+                    y = y2p.tile([P, 4, DH], F32, name="y2", tag="y2")
+                    yv = y[:]
+                view = ps2[:].rearrange("p (h c) -> p h c", h=4)
+                if w < 2:
+                    nc.scalar.mul(out=yv, in_=view, mul=Q_SCALE)
+                else:
+                    nc.scalar.copy(out=yv, in_=view)
+                if tau < 12:
+                    if jt == 2:
+                        nc.sync.dma_start(
+                            out=out_t[b, 4 * s : 4 * s + 4, 0:N1, :].rearrange("h (p j) c -> p h (j c)", j=3),
+                            in_=y[:].rearrange("p h j c -> p h (j c)"),
+                        )
+                else:
+                    nc.sync.dma_start(
+                        out=out_t[b, 4 * s : 4 * s + 4, N1:512, :].rearrange("h p c -> p h c"),
+                        in_=y[:],
+                    )
 
         w_regroup(0, 0, "v")
         w_regroup(0, 1, "v")
         w_quantise(0)
         xg0 = x_transposes(0, "ssss")
+
+        bt32 = const.tile([P, P], F32, name="bt32")
+        nc.vector.tensor_copy(out=bt32[:], in_=btile[:])
+        pb = ps2p.tile([P, 512], F32, name="ps2", tag="ps2")
+        nc.tensor.transpose(pb[:, 0:P], bt32[:], ident[:])
+        bcol = const.tile([P, 32], F32, name="bcol")
+        nc.scalar.copy(out=bcol[:], in_=pb[:, 0:32])
+
+        c32 = const.tile([P, 4, DH], F32, name="c32")
+        nc.vector.tensor_copy(out=c32[:], in_=ctr[:])
+        s32 = const.tile([P, 4, DH // 2, 2], F32, name="s32")
+        spair = strw[:].rearrange("p s (j e) -> p s j e", e=2)
+        nc.vector.tensor_copy(out=s32[:, :, :, 0], in_=spair[:, :, :, 1])
+        nc.vector.tensor_scalar_mul(out=s32[:, :, :, 1], in0=spair[:, :, :, 0], scalar1=-1.0)
+        ct1 = const.tile([P, 6 * P], F32, name="ct1")
+        ct2 = const.tile([P, P], F32, name="ct2")
+        st1 = const.tile([P, 6 * P], F32, name="st1")
+        st2 = const.tile([P, P], F32, name="st2")
+        for table, long_table, short_table in (
+            (c32[:], ct1, ct2),
+            (s32[:].rearrange("p s j e -> p s (j e)"), st1, st2),
+        ):
+            pt = ps2p.tile([P, 512], F32, name="ps2", tag="ps2")
+            for slot in range(4):
+                nc.tensor.transpose(pt[:, P * slot : P * slot + P], table[:, slot, :], ident[:])
+            nc.scalar.copy(out=long_table[:, 0:384], in_=pt[:, 0:384])
+            nc.scalar.copy(out=long_table[:, 384:768], in_=pt[:, 0:384])
+            nc.scalar.copy(out=short_table[:], in_=pt[:, 384:512])
+
         x_quantise(0, xg0)
-        xg1 = x_transposes(1, "ssvv")
         project(0)
+        xg1 = x_transposes(1, "ssss")
+        products(0, 0)
+        products(0, 1)
         x_quantise(1, xg1)
+        products(0, 2)
+        products(0, 3)
 
         jobs = [(sl, g) for sl in range(1, 8) for g in range(2)]
         quantise_after = {1: 1, 4: 2, 6: 3, 8: 4, 10: 5, 12: 6, 13: 7}
         xg_late = {}
         for i in range(n_rounds):
-            back_transposes(i)
-            if i == 0:
-                xg_late[0] = (2, x_transposes(2, "ssss"))
+            if i == 2:
+                wraw[3] = raw.tile([P, 2, 4, D], BF16, name="wraw3", tag="wraw0")
+                load_w_full(3)
             if i + 1 < n_rounds:
                 project(i + 1)
+            finish(i)
+            if i == 0:
+                xg_late[0] = (2, x_transposes(2, "ssss"))
             if i == 6:
                 xg_late[7] = (3, x_transposes(3, "ssss"))
             if i < len(jobs):
                 w_regroup(jobs[i][0], jobs[i][1], "s")
-            for tl in range(4):
-                rope(i, tl)
-            if i in xg_late:
-                x_quantise(xg_late[i][0], xg_late[i][1])
+            if i + 1 < n_rounds:
+                for hh in range(4):
+                    products(i + 1, hh)
+                    if hh == 1 and i in xg_late:
+                        x_quantise(xg_late[i][0], xg_late[i][1])
             if i in quantise_after:
                 w_quantise(quantise_after[i])

@@ -10,6 +10,7 @@ U8 = mybir.dt.uint8
 FP8X4 = mybir.dt.float8_e4m3fn_x4
 MULT = mybir.AluOpType.mult
 ADD = mybir.AluOpType.add
+IDENTITY = mybir.ActivationFunctionType.Identity
 
 P = 128
 D = 1024
@@ -46,6 +47,7 @@ def tile_dualmultiheadattention_pa_kernel(
         wgp = ctx.enter_context(tc.tile_pool(name="wgp", bufs=2))
         wcp = ctx.enter_context(tc.tile_pool(name="wcp", bufs=4))
         abp = ctx.enter_context(tc.tile_pool(name="abp", bufs=8))
+        up = ctx.enter_context(tc.tile_pool(name="up", bufs=2))
         y1p = ctx.enter_context(tc.tile_pool(name="y1p", bufs=3))
         y2p = ctx.enter_context(tc.tile_pool(name="y2p", bufs=3))
         ps1p = ctx.enter_context(tc.psum_pool(name="ps1p", bufs=4))
@@ -141,8 +143,14 @@ def tile_dualmultiheadattention_pa_kernel(
             dst = wg_tiles[sl][:, g, :, :].rearrange("p (c i) t -> p c t i", i=4)
             if engine == "s":
                 nc.scalar.copy(out=dst, in_=src)
-            else:
+            elif engine == "v":
                 nc.vector.tensor_copy(out=dst, in_=src)
+            else:
+                nc.gpsimd.tensor_scalar(
+                    out=wg_tiles[sl][:, g, :, :],
+                    in0=wraw[w][:, g, :, 512 * s : 512 * s + 512].rearrange("p t c -> p c t"),
+                    scalar1=1.0, scalar2=0.0, op0=MULT, op1=ADD,
+                )
 
         def w_quantise(sl):
             wc = wcp.tile([P, 2, 512], U32, name="wc", tag="wc", align_bytes=64)
@@ -183,6 +191,25 @@ def tile_dualmultiheadattention_pa_kernel(
             col = 8 * w + 4 * s + hh
             ps = ps1_tiles[r][hh]
             pair = []
+            if hh == 0:
+                u = up.tile([P, 512], F32, name="u", tag="u")
+                nc.scalar.activation(out=u[:], in_=ps[:], func=IDENTITY, bias=bcol[:, col : col + 1], scale=1.0)
+                for name, long_table, short_table in (("a", ct1, ct2), ("b", st1, st2)):
+                    t = abp.tile([P, 512], F32, name=name, tag=name)
+                    if grp < 3:
+                        nc.gpsimd.tensor_tensor(
+                            out=t[:], in0=u[:], in1=long_table[:, P * grp : P * grp + 512], op=MULT
+                        )
+                    else:
+                        nc.gpsimd.tensor_tensor(
+                            out=t[:].rearrange("p (t n) -> p t n", t=4),
+                            in0=u[:].rearrange("p (t n) -> p t n", t=4),
+                            in1=short_table[:].unsqueeze(1).to_broadcast([P, 4, P]),
+                            op=MULT,
+                        )
+                    pair.append(t)
+                ab_tiles[r].append(pair)
+                return
             for name, long_table, short_table in (("a", ct1, ct2), ("b", st1, st2)):
                 t = abp.tile([P, 512], F32, name=name, tag=name)
                 if grp < 3:
@@ -247,11 +274,6 @@ def tile_dualmultiheadattention_pa_kernel(
                         in_=y[:],
                     )
 
-        w_regroup(0, 0, "v")
-        w_regroup(0, 1, "v")
-        w_quantise(0)
-        xg0 = x_transposes(0, "ssss")
-
         bt32 = const.tile([P, P], F32, name="bt32")
         nc.vector.tensor_copy(out=bt32[:], in_=btile[:])
         pb = ps2p.tile([P, 512], F32, name="ps2", tag="ps2")
@@ -280,9 +302,13 @@ def tile_dualmultiheadattention_pa_kernel(
             nc.scalar.copy(out=long_table[:, 384:768], in_=pt[:, 0:384])
             nc.scalar.copy(out=short_table[:], in_=pt[:, 384:512])
 
+        w_regroup(0, 0, "v")
+        w_regroup(0, 1, "v")
+        w_quantise(0)
+        xg0 = x_transposes(0, "sssv")
         x_quantise(0, xg0)
-        project(0)
         xg1 = x_transposes(1, "ssss")
+        project(0)
         products(0, 0)
         products(0, 1)
         x_quantise(1, xg1)
@@ -290,6 +316,7 @@ def tile_dualmultiheadattention_pa_kernel(
         products(0, 3)
 
         jobs = [(sl, g) for sl in range(1, 8) for g in range(2)]
+        job_engine = "ggsggsgggsggsg"
         quantise_after = {1: 1, 4: 2, 6: 3, 8: 4, 10: 5, 12: 6, 13: 7}
         xg_late = {}
         for i in range(n_rounds):
@@ -298,15 +325,16 @@ def tile_dualmultiheadattention_pa_kernel(
                 load_w_full(3)
             if i + 1 < n_rounds:
                 project(i + 1)
+                products(i + 1, 0)
             finish(i)
             if i == 0:
                 xg_late[0] = (2, x_transposes(2, "ssss"))
             if i == 6:
                 xg_late[7] = (3, x_transposes(3, "ssss"))
             if i < len(jobs):
-                w_regroup(jobs[i][0], jobs[i][1], "s")
+                w_regroup(jobs[i][0], jobs[i][1], job_engine[i])
             if i + 1 < n_rounds:
-                for hh in range(4):
+                for hh in range(1, 4):
                     products(i + 1, hh)
                     if hh == 1 and i in xg_late:
                         x_quantise(xg_late[i][0], xg_late[i][1])

@@ -316,7 +316,7 @@ def tile_dualmultiheadattention_pa_kernel(
         products(0, 3)
 
         jobs = [(sl, g) for sl in range(1, 8) for g in range(2)]
-        job_engine = "ggsggsgggsggsg"
+        job_engine = "gsgsgsgsgsgsgs"
         quantise_after = {1: 1, 4: 2, 6: 3, 8: 4, 10: 5, 12: 6, 13: 7}
         xg_late = {}
         for i in range(n_rounds):

@@ -14,6 +14,7 @@ IDENTITY = mybir.ActivationFunctionType.Identity
 
 P = 128
 D = 1024
+HEADS = 8
 DH = 128
 N1 = 384
 Q_SCALE = DH ** -0.5
@@ -46,35 +47,28 @@ def tile_dualmultiheadattention_pa_kernel(
         xgp = ctx.enter_context(tc.tile_pool(name="xgp", bufs=2))
         wgp = ctx.enter_context(tc.tile_pool(name="wgp", bufs=2))
         wcp = ctx.enter_context(tc.tile_pool(name="wcp", bufs=4))
-        abp = ctx.enter_context(tc.tile_pool(name="abp", bufs=8))
-        up = ctx.enter_context(tc.tile_pool(name="up", bufs=2))
+        up = ctx.enter_context(tc.tile_pool(name="up", bufs=8))
+        abp = ctx.enter_context(tc.tile_pool(name="abp", bufs=3))
         y1p = ctx.enter_context(tc.tile_pool(name="y1p", bufs=3))
         y2p = ctx.enter_context(tc.tile_pool(name="y2p", bufs=3))
-        ps1p = ctx.enter_context(tc.psum_pool(name="ps1p", bufs=4))
-        ps2p = ctx.enter_context(tc.psum_pool(name="ps2p", bufs=4))
+        ps1p = ctx.enter_context(tc.psum_pool(name="ps1p", bufs=3))
+        ps2p = ctx.enter_context(tc.psum_pool(name="ps2p", bufs=5))
         if MANUAL:
             ctx.enter_context(tc.manual_schedule())
 
         ident = const.tile([P, P], F32, name="ident")
         masks.make_identity(nc, ident[:])
-        pswap = const.tile([P, P], F32, name="pswap")
-        for e in range(2):
-            nc.gpsimd.tensor_copy(
-                out=pswap[:].rearrange("p (j e) -> p j e", e=2)[:, :, e],
-                in_=ident[:].rearrange("p (j e) -> p j e", e=2)[:, :, 1 - e],
-            )
 
         x1r = [raw.tile([P, 3, D], BF16, name="x1r%d" % b) for b in range(4)]
         x2r = raw.tile([P, 4, D], BF16, name="x2r")
-        wraw = {}
-        for w in (0, 2, 1):
-            wraw[w] = raw.tile([P, 2, 4, D], BF16, name="wraw%d" % w)
+        whalf = [raw.tile([P, 2, 4, 512], BF16, name="whalf%d" % s) for s in range(2)]
+        wraw = [None] + [raw.tile([P, 2, 4, D], BF16, name="wraw%d" % w) for w in range(1, 4)]
 
-        def load_w(w, c0, c1):
-            src = weights[w].rearrange("(m q e) c -> q m e c", m=4, e=2)
-            dst = wraw[w][:].rearrange("q g (u e) c -> q (g u) e c", e=2)
+        def load_w_half(s):
+            src = wq1.rearrange("(m q e) c -> q m e c", m=4, e=2)
+            dst = whalf[s][:].rearrange("q g (u e) c -> q (g u) e c", e=2)
             for e in range(2):
-                nc.sync.dma_start(out=dst[:, :, e, c0:c1], in_=src[:, :, e, c0:c1])
+                nc.sync.dma_start(out=dst[:, :, e, :], in_=src[:, :, e, 512 * s : 512 * s + 512])
 
         def load_w_full(w):
             nc.sync.dma_start(
@@ -82,24 +76,40 @@ def tile_dualmultiheadattention_pa_kernel(
                 in_=weights[w].rearrange("(m q e) c -> q m (e c)", m=4, e=2),
             )
 
-        load_w(0, 0, 512)
-        for b in range(4):
-            nc.sync.dma_start(out=x1r[b][:], in_=x_1[b].rearrange("(p j) k -> p j k", j=3))
-        load_w(0, 512, 1024)
-        load_w_full(2)
-        nc.sync.dma_start(out=x2r[:], in_=x_2.rearrange("b p k -> p b k"))
-        load_w_full(1)
-
         btile = const.tile([P, P], BF16, name="btile")
         nc.vector.memset(btile[:], 0.0)
-        for w in range(4):
-            nc.scalar.dma_start(out=btile[8 * w : 8 * w + 8, :], in_=biases[w].rearrange("(h c) -> h c", c=DH))
         ctr = const.tile([P, 4, DH], BF16, name="ctr")
         strw = const.tile([P, 4, DH], BF16, name="strw")
+        for w in range(4):
+            nc.scalar.dma_start(out=btile[8 * w : 8 * w + 8, :], in_=biases[w].rearrange("(h c) -> h c", c=DH))
         nc.scalar.dma_start(out=ctr[:, 0:3, :], in_=cos1.rearrange("(p j) c -> p j c", j=3))
-        nc.scalar.dma_start(out=ctr[:, 3, :], in_=cos2)
         nc.scalar.dma_start(out=strw[:, 0:3, :], in_=sin1.rearrange("(p j) c -> p j c", j=3))
-        nc.scalar.dma_start(out=strw[:, 3, :], in_=sin2)
+        load_w_half(0)
+        for b in range(4):
+            nc.sync.dma_start(out=x1r[b][:], in_=x_1[b].rearrange("(p j) k -> p j k", j=3))
+        load_w_half(1)
+        load_w_full(2)
+        nc.sync.dma_start(out=x2r[:], in_=x_2.rearrange("b p k -> p b k"))
+        nc.sync.dma_start(out=ctr[:, 3, :], in_=cos2)
+        nc.sync.dma_start(out=strw[:, 3, :], in_=sin2)
+        load_w_full(1)
+        load_w_full(3)
+
+        bt32 = const.tile([P, P], F32, name="bt32")
+        bcol = const.tile([P, 32], F32, name="bcol")
+        ctab = const.tile([P, 4, DH], F32, name="ctab")
+        stab = const.tile([P, 4, 2, DH // 2], F32, name="stab")
+        spair = strw[:].rearrange("p s (j e) -> p s j e", e=2)
+        nc.gpsimd.tensor_copy(out=bt32[:], in_=btile[:])
+
+        def cast_tables(lo, hi):
+            nc.gpsimd.tensor_copy(out=ctab[:, lo:hi, :], in_=ctr[:, lo:hi, :])
+            nc.gpsimd.tensor_scalar(
+                out=stab[:, lo:hi, 0, :], in0=spair[:, lo:hi, :, 0], scalar1=-1.0, scalar2=0.0, op0=MULT, op1=ADD
+            )
+            nc.gpsimd.tensor_copy(out=stab[:, lo:hi, 1, :], in_=spair[:, lo:hi, :, 1])
+
+        cast_tables(0, 3)
 
         xc = [const.tile([P, 2, 512], U32, name="xc%d" % g, align_bytes=64) for g in range(4)]
         xs = [const.tile([P, 2, 512], U8, name="xs%d" % g, align_bytes=64) for g in range(4)]
@@ -113,7 +123,7 @@ def tile_dualmultiheadattention_pa_kernel(
                     src = x1r[tau // 3][:, tau % 3, :].bitcast(F32)
                 else:
                     src = x2r[:, tau - 12, :].bitcast(F32)
-                xt = ps2p.tile([P, 512], F32, name="ps2", tag="ps2")
+                xt = ps1p.tile([P, 512], F32, name="ps1", tag="ps1")
                 for m in range(4):
                     nc.tensor.transpose(xt[:, P * m : P * m + P], src[:, P * m : P * m + P], ident[:])
                 dst = xg32[:, :, P * tl : P * tl + P, :]
@@ -139,18 +149,16 @@ def tile_dualmultiheadattention_pa_kernel(
             w, s = SLICES[sl]
             if g == 0:
                 wg_tiles[sl] = wgp.tile([P, 2, 512, 4], BF16, name="wg", tag="wg", align_bytes=64)
-            src = wraw[w][:, g, :, 512 * s : 512 * s + 512].rearrange("p t (c i) -> p c t i", i=4)
+            if w == 0:
+                rows = whalf[s][:, g, :, :]
+            else:
+                rows = wraw[w][:, g, :, 512 * s : 512 * s + 512]
+            src = rows.rearrange("p t (c i) -> p c t i", i=4)
             dst = wg_tiles[sl][:, g, :, :].rearrange("p (c i) t -> p c t i", i=4)
             if engine == "s":
                 nc.scalar.copy(out=dst, in_=src)
-            elif engine == "v":
-                nc.vector.tensor_copy(out=dst, in_=src)
             else:
-                nc.gpsimd.tensor_scalar(
-                    out=wg_tiles[sl][:, g, :, :],
-                    in0=wraw[w][:, g, :, 512 * s : 512 * s + 512].rearrange("p t c -> p c t"),
-                    scalar1=1.0, scalar2=0.0, op0=MULT, op1=ADD,
-                )
+                nc.vector.tensor_copy(out=dst, in_=src)
 
         def w_quantise(sl):
             wc = wcp.tile([P, 2, 512], U32, name="wc", tag="wc", align_bytes=64)
@@ -162,13 +170,14 @@ def tile_dualmultiheadattention_pa_kernel(
             )
             w_codes[sl] = (wc, ws)
 
-        ps1_tiles = {}
-        ab_tiles = {}
+        u_tiles = {}
 
         def project(r):
             sl, grp = rounds[r]
+            w, s = SLICES[sl]
             wc, ws = w_codes[sl]
-            banks = []
+            scale = Q_SCALE if w < 2 else 1.0
+            us = []
             for hh in range(4):
                 ps = ps1p.tile([P, 512], F32, name="ps1", tag="ps1")
                 for g in range(2):
@@ -181,162 +190,108 @@ def tile_dualmultiheadattention_pa_kernel(
                         start=(g == 0),
                         stop=(g == 1),
                     )
-                banks.append(ps)
-            ps1_tiles[r] = banks
-            ab_tiles[r] = []
-
-        def products(r, hh):
-            sl, grp = rounds[r]
-            w, s = SLICES[sl]
-            col = 8 * w + 4 * s + hh
-            ps = ps1_tiles[r][hh]
-            pair = []
-            if hh == 0:
                 u = up.tile([P, 512], F32, name="u", tag="u")
-                nc.scalar.activation(out=u[:], in_=ps[:], func=IDENTITY, bias=bcol[:, col : col + 1], scale=1.0)
-                for name, long_table, short_table in (("a", ct1, ct2), ("b", st1, st2)):
-                    t = abp.tile([P, 512], F32, name=name, tag=name)
-                    if grp < 3:
-                        nc.gpsimd.tensor_tensor(
-                            out=t[:], in0=u[:], in1=long_table[:, P * grp : P * grp + 512], op=MULT
-                        )
-                    else:
-                        nc.gpsimd.tensor_tensor(
-                            out=t[:].rearrange("p (t n) -> p t n", t=4),
-                            in0=u[:].rearrange("p (t n) -> p t n", t=4),
-                            in1=short_table[:].unsqueeze(1).to_broadcast([P, 4, P]),
-                            op=MULT,
-                        )
-                    pair.append(t)
-                ab_tiles[r].append(pair)
-                return
-            for name, long_table, short_table in (("a", ct1, ct2), ("b", st1, st2)):
-                t = abp.tile([P, 512], F32, name=name, tag=name)
-                if grp < 3:
-                    nc.vector.scalar_tensor_tensor(
-                        out=t[:], in0=ps[:], scalar=bcol[:, col : col + 1],
-                        in1=long_table[:, P * grp : P * grp + 512], op0=ADD, op1=MULT,
-                    )
-                else:
-                    nc.vector.scalar_tensor_tensor(
-                        out=t[:].rearrange("p (t n) -> p t n", t=4),
-                        in0=ps[:].rearrange("p (t n) -> p t n", t=4),
-                        scalar=bcol[:, col : col + 1],
-                        in1=short_table[:].unsqueeze(1).to_broadcast([P, 4, P]),
-                        op0=ADD, op1=MULT,
-                    )
-                pair.append(t)
-            ab_tiles[r].append(pair)
+                col = 8 * w + 4 * s + hh
+                nc.scalar.activation(out=u[:], in_=ps[:], func=IDENTITY, bias=bcol[:, col : col + 1], scale=scale)
+                us.append(u)
+            u_tiles[r] = us
 
         y_open = {}
+        ps2_tiles = {}
 
-        def finish(r):
+        def back_transposes(r):
+            us = u_tiles[r]
+            banks = []
+            for tl in range(4):
+                ps2 = ps2p.tile([P, 512], F32, name="ps2", tag="ps2")
+                for hh in range(4):
+                    nc.tensor.transpose(ps2[:, P * hh : P * hh + P], us[hh][:, P * tl : P * tl + P], ident[:])
+                banks.append(ps2)
+            ps2_tiles[r] = banks
+
+        def rope(r, tl):
             sl, grp = rounds[r]
             w, s = SLICES[sl]
             out_t = outs[w]
-            for tl in range(4):
-                tau = 4 * grp + tl
-                ps2 = ps2p.tile([P, 512], F32, name="ps2", tag="ps2")
-                for hh in range(4):
-                    a, b2 = ab_tiles[r][hh]
-                    nc.tensor.matmul(
-                        out=ps2[:, P * hh : P * hh + P], lhsT=a[:, P * tl : P * tl + P], rhs=ident[:],
-                        start=True, stop=False, is_transpose=True,
-                    )
-                    nc.tensor.matmul(
-                        out=ps2[:, P * hh : P * hh + P], lhsT=b2[:, P * tl : P * tl + P], rhs=pswap[:],
-                        start=False, stop=True, is_transpose=True,
-                    )
-                if tau < 12:
-                    b, jt = tau // 3, tau % 3
-                    if jt == 0:
-                        y_open[b] = y1p.tile([P, 4, 3, DH], F32, name="y1", tag="y1")
-                    y = y_open[b]
-                    yv = y[:, :, jt, :]
-                else:
-                    b, jt = tau - 12, 0
-                    y = y2p.tile([P, 4, DH], F32, name="y2", tag="y2")
-                    yv = y[:]
-                view = ps2[:].rearrange("p (h c) -> p h c", h=4)
-                if w < 2:
-                    nc.scalar.mul(out=yv, in_=view, mul=Q_SCALE)
-                else:
-                    nc.scalar.copy(out=yv, in_=view)
-                if tau < 12:
-                    if jt == 2:
-                        nc.sync.dma_start(
-                            out=out_t[b, 4 * s : 4 * s + 4, 0:N1, :].rearrange("h (p j) c -> p h (j c)", j=3),
-                            in_=y[:].rearrange("p h j c -> p h (j c)"),
-                        )
-                else:
+            tau = 4 * grp + tl
+            ps2 = ps2_tiles[r][tl]
+            slot = tau % 3 if tau < 12 else 3
+            a = abp.tile([P, 4, DH], F32, name="a", tag="a")
+            nc.vector.tensor_tensor(
+                out=a[:],
+                in0=ps2[:].rearrange("p (h c) -> p h c", h=4),
+                in1=ctab[:, slot, :].unsqueeze(1).to_broadcast([P, 4, DH]),
+                op=MULT,
+            )
+            bt = abp.tile([P, 2, 4, DH // 2], F32, name="bt", tag="bt")
+            pairs = ps2[:].rearrange("p (h j e) -> p h j e", h=4, e=2)
+            for e in range(2):
+                nc.vector.tensor_tensor(
+                    out=bt[:, e, :, :],
+                    in0=pairs[:, :, :, 1 - e],
+                    in1=stab[:, slot, e, :].unsqueeze(1).to_broadcast([P, 4, DH // 2]),
+                    op=MULT,
+                )
+            if tau < 12:
+                b, jt = tau // 3, tau % 3
+                if jt == 0:
+                    y_open[b] = y1p.tile([P, 4, 3, DH], F32, name="y1", tag="y1")
+                y = y_open[b]
+                yv = y[:, :, jt, :]
+            else:
+                b, jt = tau - 12, 0
+                y = y2p.tile([P, 4, DH], F32, name="y2", tag="y2")
+                yv = y[:]
+            adder = nc.vector if (r % 2 == 1 and tl == 3) else nc.gpsimd
+            adder.tensor_tensor(
+                out=yv.rearrange("p h (j e) -> p h j e", e=2),
+                in0=a[:].rearrange("p h (j e) -> p h j e", e=2),
+                in1=bt[:].rearrange("p e h j -> p h j e"),
+                op=ADD,
+            )
+            if tau < 12:
+                if jt == 2:
                     nc.sync.dma_start(
-                        out=out_t[b, 4 * s : 4 * s + 4, N1:512, :].rearrange("h p c -> p h c"),
-                        in_=y[:],
+                        out=out_t[b, 4 * s : 4 * s + 4, 0:N1, :].rearrange("h (p j) c -> p h (j c)", j=3),
+                        in_=y[:].rearrange("p h j c -> p h (j c)"),
                     )
-
-        bt32 = const.tile([P, P], F32, name="bt32")
-        nc.vector.tensor_copy(out=bt32[:], in_=btile[:])
-        pb = ps2p.tile([P, 512], F32, name="ps2", tag="ps2")
-        nc.tensor.transpose(pb[:, 0:P], bt32[:], ident[:])
-        bcol = const.tile([P, 32], F32, name="bcol")
-        nc.scalar.copy(out=bcol[:], in_=pb[:, 0:32])
-
-        c32 = const.tile([P, 4, DH], F32, name="c32")
-        nc.vector.tensor_copy(out=c32[:], in_=ctr[:])
-        s32 = const.tile([P, 4, DH // 2, 2], F32, name="s32")
-        spair = strw[:].rearrange("p s (j e) -> p s j e", e=2)
-        nc.vector.tensor_copy(out=s32[:, :, :, 0], in_=spair[:, :, :, 1])
-        nc.vector.tensor_scalar_mul(out=s32[:, :, :, 1], in0=spair[:, :, :, 0], scalar1=-1.0)
-        ct1 = const.tile([P, 6 * P], F32, name="ct1")
-        ct2 = const.tile([P, P], F32, name="ct2")
-        st1 = const.tile([P, 6 * P], F32, name="st1")
-        st2 = const.tile([P, P], F32, name="st2")
-        for table, long_table, short_table in (
-            (c32[:], ct1, ct2),
-            (s32[:].rearrange("p s j e -> p s (j e)"), st1, st2),
-        ):
-            pt = ps2p.tile([P, 512], F32, name="ps2", tag="ps2")
-            for slot in range(4):
-                nc.tensor.transpose(pt[:, P * slot : P * slot + P], table[:, slot, :], ident[:])
-            nc.scalar.copy(out=long_table[:, 0:384], in_=pt[:, 0:384])
-            nc.scalar.copy(out=long_table[:, 384:768], in_=pt[:, 0:384])
-            nc.scalar.copy(out=short_table[:], in_=pt[:, 384:512])
+            else:
+                nc.sync.dma_start(
+                    out=out_t[b, 4 * s : 4 * s + 4, N1:512, :].rearrange("h p c -> p h c"),
+                    in_=y[:],
+                )
 
         w_regroup(0, 0, "v")
         w_regroup(0, 1, "v")
         w_quantise(0)
-        xg0 = x_transposes(0, "sssv")
+        xg0 = x_transposes(0, "ssss")
         x_quantise(0, xg0)
-        xg1 = x_transposes(1, "ssss")
+        pb = ps2p.tile([P, 512], F32, name="ps2", tag="ps2")
+        nc.tensor.transpose(pb[:, 0:P], bt32[:], ident[:])
+        nc.scalar.mul(out=bcol[:, 0:16], in_=pb[:, 0:16], mul=Q_SCALE)
+        nc.scalar.copy(out=bcol[:, 16:32], in_=pb[:, 16:32])
+        xg1 = x_transposes(1, "ssvv")
         project(0)
-        products(0, 0)
-        products(0, 1)
         x_quantise(1, xg1)
-        products(0, 2)
-        products(0, 3)
 
         jobs = [(sl, g) for sl in range(1, 8) for g in range(2)]
-        job_engine = "gsgsgsgsgsgsgs"
         quantise_after = {1: 1, 4: 2, 6: 3, 8: 4, 10: 5, 12: 6, 13: 7}
         xg_late = {}
         for i in range(n_rounds):
-            if i == 2:
-                wraw[3] = raw.tile([P, 2, 4, D], BF16, name="wraw3", tag="wraw0")
-                load_w_full(3)
-            if i + 1 < n_rounds:
-                project(i + 1)
-                products(i + 1, 0)
-            finish(i)
+            back_transposes(i)
             if i == 0:
                 xg_late[0] = (2, x_transposes(2, "ssss"))
+            if i + 1 < n_rounds:
+                project(i + 1)
+            if i == 4:
+                cast_tables(3, 4)
             if i == 6:
                 xg_late[7] = (3, x_transposes(3, "ssss"))
             if i < len(jobs):
-                w_regroup(jobs[i][0], jobs[i][1], job_engine[i])
-            if i + 1 < n_rounds:
-                for hh in range(1, 4):
-                    products(i + 1, hh)
-                    if hh == 1 and i in xg_late:
-                        x_quantise(xg_late[i][0], xg_late[i][1])
+                w_regroup(jobs[i][0], jobs[i][1], "s")
+            for tl in range(4):
+                rope(i, tl)
+            if i in xg_late:
+                x_quantise(xg_late[i][0], xg_late[i][1])
             if i in quantise_after:
                 w_quantise(quantise_after[i])

@@ -14,7 +14,6 @@ IDENTITY = mybir.ActivationFunctionType.Identity
 
 P = 128
 D = 1024
-HEADS = 8
 DH = 128
 N1 = 384
 Q_SCALE = DH ** -0.5
@@ -30,7 +29,6 @@ def tile_dualmultiheadattention_pa_kernel(
 ):
     nc = tc.nc
     weights = [wq1, wq2, wk1, wk2]
-    biases = [bq1, bq2, bk1, bk2]
     outs = [out_0, out_0, out_1, out_1]
 
     rounds = []
@@ -47,26 +45,40 @@ def tile_dualmultiheadattention_pa_kernel(
         xgp = ctx.enter_context(tc.tile_pool(name="xgp", bufs=2))
         wgp = ctx.enter_context(tc.tile_pool(name="wgp", bufs=2))
         wcp = ctx.enter_context(tc.tile_pool(name="wcp", bufs=4))
-        up = ctx.enter_context(tc.tile_pool(name="up", bufs=8))
-        abp = ctx.enter_context(tc.tile_pool(name="abp", bufs=3))
+        abp = ctx.enter_context(tc.tile_pool(name="abp", bufs=8))
+        up = ctx.enter_context(tc.tile_pool(name="up", bufs=2))
         y1p = ctx.enter_context(tc.tile_pool(name="y1p", bufs=3))
         y2p = ctx.enter_context(tc.tile_pool(name="y2p", bufs=3))
-        ps1p = ctx.enter_context(tc.psum_pool(name="ps1p", bufs=3))
-        ps2p = ctx.enter_context(tc.psum_pool(name="ps2p", bufs=5))
+        ps1p = ctx.enter_context(tc.psum_pool(name="ps1p", bufs=4))
+        ps2p = ctx.enter_context(tc.psum_pool(name="ps2p", bufs=4))
         if MANUAL:
             ctx.enter_context(tc.manual_schedule())
 
         ident = const.tile([P, P], F32, name="ident")
         masks.make_identity(nc, ident[:])
+        pswap = const.tile([P, P], F32, name="pswap")
+        for e in range(2):
+            nc.gpsimd.tensor_copy(
+                out=pswap[:].rearrange("p (j e) -> p j e", e=2)[:, :, e],
+                in_=ident[:].rearrange("p (j e) -> p j e", e=2)[:, :, 1 - e],
+            )
 
         x1r = [raw.tile([P, 3, D], BF16, name="x1r%d" % b) for b in range(4)]
         x2r = raw.tile([P, 4, D], BF16, name="x2r")
-        whalf = [raw.tile([P, 2, 4, 512], BF16, name="whalf%d" % s) for s in range(2)]
-        wraw = [None] + [raw.tile([P, 2, 4, D], BF16, name="wraw%d" % w) for w in range(1, 4)]
+        whalf = {}
+        wraw = {}
+        for w in (2, 1):
+            wraw[w] = raw.tile([P, 2, 4, D], BF16, name="wraw%d" % w)
 
-        def load_w_half(s):
-            src = wq1.rearrange("(m q e) c -> q m e c", m=4, e=2)
-            dst = whalf[s][:].rearrange("q g (u e) c -> q (g u) e c", e=2)
+        def load_w_halves(w):
+            whalf[w] = []
+            for s in range(2):
+                half_tile = raw.tile([P, 2, 4, 512], BF16, name="whalf%d" % s, tag="whalf%d" % s)
+                whalf[w].append(half_tile)
+
+        def load_w_half(w, s):
+            src = weights[w].rearrange("(m q e) c -> q m e c", m=4, e=2)
+            dst = whalf[w][s][:].rearrange("q g (u e) c -> q (g u) e c", e=2)
             for e in range(2):
                 nc.sync.dma_start(out=dst[:, :, e, :], in_=src[:, :, e, 512 * s : 512 * s + 512])
 
@@ -76,40 +88,29 @@ def tile_dualmultiheadattention_pa_kernel(
                 in_=weights[w].rearrange("(m q e) c -> q m (e c)", m=4, e=2),
             )
 
-        btile = const.tile([P, P], BF16, name="btile")
-        nc.vector.memset(btile[:], 0.0)
+        btile = [const.tile([P, P], BF16, name="btile%d" % st) for st in range(2)]
         ctr = const.tile([P, 4, DH], BF16, name="ctr")
         strw = const.tile([P, 4, DH], BF16, name="strw")
-        for w in range(4):
-            nc.scalar.dma_start(out=btile[8 * w : 8 * w + 8, :], in_=biases[w].rearrange("(h c) -> h c", c=DH))
+        for st in range(2):
+            nc.vector.memset(btile[st][:], 0.0)
         nc.scalar.dma_start(out=ctr[:, 0:3, :], in_=cos1.rearrange("(p j) c -> p j c", j=3))
         nc.scalar.dma_start(out=strw[:, 0:3, :], in_=sin1.rearrange("(p j) c -> p j c", j=3))
-        load_w_half(0)
-        for b in range(4):
+        nc.scalar.dma_start(out=btile[0][0:8, :], in_=bq1.rearrange("(h c) -> h c", c=DH))
+        nc.scalar.dma_start(out=btile[0][8:16, :], in_=bk1.rearrange("(h c) -> h c", c=DH))
+        load_w_halves(0)
+        load_w_half(0, 0)
+        for b in range(2):
             nc.sync.dma_start(out=x1r[b][:], in_=x_1[b].rearrange("(p j) k -> p j k", j=3))
-        load_w_half(1)
+        for b in range(2, 4):
+            nc.sync.dma_start(out=x1r[b][:], in_=x_1[b].rearrange("(p j) k -> p j k", j=3))
+        load_w_half(0, 1)
         load_w_full(2)
         nc.sync.dma_start(out=x2r[:], in_=x_2.rearrange("b p k -> p b k"))
         nc.sync.dma_start(out=ctr[:, 3, :], in_=cos2)
         nc.sync.dma_start(out=strw[:, 3, :], in_=sin2)
+        nc.sync.dma_start(out=btile[1][0:8, :], in_=bq2.rearrange("(h c) -> h c", c=DH))
+        nc.sync.dma_start(out=btile[1][8:16, :], in_=bk2.rearrange("(h c) -> h c", c=DH))
         load_w_full(1)
-        load_w_full(3)
-
-        bt32 = const.tile([P, P], F32, name="bt32")
-        bcol = const.tile([P, 32], F32, name="bcol")
-        ctab = const.tile([P, 4, DH], F32, name="ctab")
-        stab = const.tile([P, 4, 2, DH // 2], F32, name="stab")
-        spair = strw[:].rearrange("p s (j e) -> p s j e", e=2)
-        nc.gpsimd.tensor_copy(out=bt32[:], in_=btile[:])
-
-        def cast_tables(lo, hi):
-            nc.gpsimd.tensor_copy(out=ctab[:, lo:hi, :], in_=ctr[:, lo:hi, :])
-            nc.gpsimd.tensor_scalar(
-                out=stab[:, lo:hi, 0, :], in0=spair[:, lo:hi, :, 0], scalar1=-1.0, scalar2=0.0, op0=MULT, op1=ADD
-            )
-            nc.gpsimd.tensor_copy(out=stab[:, lo:hi, 1, :], in_=spair[:, lo:hi, :, 1])
-
-        cast_tables(0, 3)
 
         xc = [const.tile([P, 2, 512], U32, name="xc%d" % g, align_bytes=64) for g in range(4)]
         xs = [const.tile([P, 2, 512], U8, name="xs%d" % g, align_bytes=64) for g in range(4)]
@@ -123,7 +124,7 @@ def tile_dualmultiheadattention_pa_kernel(
                     src = x1r[tau // 3][:, tau % 3, :].bitcast(F32)
                 else:
                     src = x2r[:, tau - 12, :].bitcast(F32)
-                xt = ps1p.tile([P, 512], F32, name="ps1", tag="ps1")
+                xt = ps2p.tile([P, 512], F32, name="ps2", tag="ps2")
                 for m in range(4):
                     nc.tensor.transpose(xt[:, P * m : P * m + P], src[:, P * m : P * m + P], ident[:])
                 dst = xg32[:, :, P * tl : P * tl + P, :]
@@ -149,16 +150,22 @@ def tile_dualmultiheadattention_pa_kernel(
             w, s = SLICES[sl]
             if g == 0:
                 wg_tiles[sl] = wgp.tile([P, 2, 512, 4], BF16, name="wg", tag="wg", align_bytes=64)
-            if w == 0:
-                rows = whalf[s][:, g, :, :]
+            if w in whalf:
+                rows = whalf[w][s][:, g, :, :]
             else:
                 rows = wraw[w][:, g, :, 512 * s : 512 * s + 512]
             src = rows.rearrange("p t (c i) -> p c t i", i=4)
             dst = wg_tiles[sl][:, g, :, :].rearrange("p (c i) t -> p c t i", i=4)
             if engine == "s":
                 nc.scalar.copy(out=dst, in_=src)
-            else:
+            elif engine == "v":
                 nc.vector.tensor_copy(out=dst, in_=src)
+            else:
+                nc.gpsimd.tensor_scalar(
+                    out=wg_tiles[sl][:, g, :, :],
+                    in0=rows.rearrange("p t c -> p c t"),
+                    scalar1=1.0, scalar2=0.0, op0=MULT, op1=ADD,
+                )
 
         def w_quantise(sl):
             wc = wcp.tile([P, 2, 512], U32, name="wc", tag="wc", align_bytes=64)
@@ -170,15 +177,17 @@ def tile_dualmultiheadattention_pa_kernel(
             )
             w_codes[sl] = (wc, ws)
 
-        u_tiles = {}
+        ps1_tiles = {}
+        ab_tiles = {}
 
-        def project(r):
+        def project(r, heads):
             sl, grp = rounds[r]
-            w, s = SLICES[sl]
             wc, ws = w_codes[sl]
-            scale = Q_SCALE if w < 2 else 1.0
-            us = []
-            for hh in range(4):
+            if r not in ps1_tiles:
+                ps1_tiles[r] = []
+                ab_tiles[r] = []
+            banks = ps1_tiles[r]
+            for hh in heads:
                 ps = ps1p.tile([P, 512], F32, name="ps1", tag="ps1")
                 for g in range(2):
                     nc.tensor.matmul_mx(
@@ -190,108 +199,172 @@ def tile_dualmultiheadattention_pa_kernel(
                         start=(g == 0),
                         stop=(g == 1),
                     )
+                banks.append(ps)
+
+        def products(r, hh):
+            sl, grp = rounds[r]
+            w, s = SLICES[sl]
+            bias = bcol[w % 2][:, 8 * (w // 2) + 4 * s + hh : 8 * (w // 2) + 4 * s + hh + 1]
+            ps = ps1_tiles[r][hh]
+            pair = []
+            if hh == 0:
                 u = up.tile([P, 512], F32, name="u", tag="u")
-                col = 8 * w + 4 * s + hh
-                nc.scalar.activation(out=u[:], in_=ps[:], func=IDENTITY, bias=bcol[:, col : col + 1], scale=scale)
-                us.append(u)
-            u_tiles[r] = us
+                nc.scalar.activation(out=u[:], in_=ps[:], func=IDENTITY, bias=bias, scale=1.0)
+                for name, long_table, short_table in (("a", ct1, ct2), ("b", st1, st2)):
+                    t = abp.tile([P, 512], F32, name=name, tag=name)
+                    if grp < 3:
+                        nc.gpsimd.tensor_tensor(
+                            out=t[:], in0=u[:], in1=long_table[:, P * grp : P * grp + 512], op=MULT
+                        )
+                    else:
+                        nc.gpsimd.tensor_tensor(
+                            out=t[:].rearrange("p (t n) -> p t n", t=4),
+                            in0=u[:].rearrange("p (t n) -> p t n", t=4),
+                            in1=short_table[:].unsqueeze(1).to_broadcast([P, 4, P]),
+                            op=MULT,
+                        )
+                    pair.append(t)
+                ab_tiles[r].append(pair)
+                return
+            for name, long_table, short_table in (("a", ct1, ct2), ("b", st1, st2)):
+                t = abp.tile([P, 512], F32, name=name, tag=name)
+                if grp < 3:
+                    nc.vector.scalar_tensor_tensor(
+                        out=t[:], in0=ps[:], scalar=bias,
+                        in1=long_table[:, P * grp : P * grp + 512], op0=ADD, op1=MULT,
+                    )
+                else:
+                    nc.vector.scalar_tensor_tensor(
+                        out=t[:].rearrange("p (t n) -> p t n", t=4),
+                        in0=ps[:].rearrange("p (t n) -> p t n", t=4),
+                        scalar=bias,
+                        in1=short_table[:].unsqueeze(1).to_broadcast([P, 4, P]),
+                        op0=ADD, op1=MULT,
+                    )
+                pair.append(t)
+            ab_tiles[r].append(pair)
 
         y_open = {}
-        ps2_tiles = {}
 
-        def back_transposes(r):
-            us = u_tiles[r]
-            banks = []
-            for tl in range(4):
-                ps2 = ps2p.tile([P, 512], F32, name="ps2", tag="ps2")
-                for hh in range(4):
-                    nc.tensor.transpose(ps2[:, P * hh : P * hh + P], us[hh][:, P * tl : P * tl + P], ident[:])
-                banks.append(ps2)
-            ps2_tiles[r] = banks
-
-        def rope(r, tl):
+        def finish(r, tiles):
             sl, grp = rounds[r]
             w, s = SLICES[sl]
             out_t = outs[w]
-            tau = 4 * grp + tl
-            ps2 = ps2_tiles[r][tl]
-            slot = tau % 3 if tau < 12 else 3
-            a = abp.tile([P, 4, DH], F32, name="a", tag="a")
-            nc.vector.tensor_tensor(
-                out=a[:],
-                in0=ps2[:].rearrange("p (h c) -> p h c", h=4),
-                in1=ctab[:, slot, :].unsqueeze(1).to_broadcast([P, 4, DH]),
-                op=MULT,
-            )
-            bt = abp.tile([P, 2, 4, DH // 2], F32, name="bt", tag="bt")
-            pairs = ps2[:].rearrange("p (h j e) -> p h j e", h=4, e=2)
-            for e in range(2):
-                nc.vector.tensor_tensor(
-                    out=bt[:, e, :, :],
-                    in0=pairs[:, :, :, 1 - e],
-                    in1=stab[:, slot, e, :].unsqueeze(1).to_broadcast([P, 4, DH // 2]),
-                    op=MULT,
-                )
-            if tau < 12:
-                b, jt = tau // 3, tau % 3
-                if jt == 0:
-                    y_open[b] = y1p.tile([P, 4, 3, DH], F32, name="y1", tag="y1")
-                y = y_open[b]
-                yv = y[:, :, jt, :]
-            else:
-                b, jt = tau - 12, 0
-                y = y2p.tile([P, 4, DH], F32, name="y2", tag="y2")
-                yv = y[:]
-            adder = nc.vector if (r % 2 == 1 and tl == 3) else nc.gpsimd
-            adder.tensor_tensor(
-                out=yv.rearrange("p h (j e) -> p h j e", e=2),
-                in0=a[:].rearrange("p h (j e) -> p h j e", e=2),
-                in1=bt[:].rearrange("p e h j -> p h j e"),
-                op=ADD,
-            )
-            if tau < 12:
-                if jt == 2:
-                    nc.sync.dma_start(
-                        out=out_t[b, 4 * s : 4 * s + 4, 0:N1, :].rearrange("h (p j) c -> p h (j c)", j=3),
-                        in_=y[:].rearrange("p h j c -> p h (j c)"),
+            for tl in tiles:
+                tau = 4 * grp + tl
+                ps2 = ps2p.tile([P, 512], F32, name="ps2", tag="ps2")
+                for hh in range(4):
+                    a, b2 = ab_tiles[r][hh]
+                    nc.tensor.matmul(
+                        out=ps2[:, P * hh : P * hh + P], lhsT=a[:, P * tl : P * tl + P], rhs=ident[:],
+                        start=True, stop=False, is_transpose=True,
                     )
-            else:
-                nc.sync.dma_start(
-                    out=out_t[b, 4 * s : 4 * s + 4, N1:512, :].rearrange("h p c -> p h c"),
-                    in_=y[:],
-                )
+                    nc.tensor.matmul(
+                        out=ps2[:, P * hh : P * hh + P], lhsT=b2[:, P * tl : P * tl + P], rhs=pswap[:],
+                        start=False, stop=True, is_transpose=True,
+                    )
+                if tau < 12:
+                    b, jt = tau // 3, tau % 3
+                    if jt == 0:
+                        y_open[b] = y1p.tile([P, 4, 3, DH], F32, name="y1", tag="y1")
+                    y = y_open[b]
+                    yv = y[:, :, jt, :]
+                else:
+                    b, jt = tau - 12, 0
+                    y = y2p.tile([P, 4, DH], F32, name="y2", tag="y2")
+                    yv = y[:]
+                view = ps2[:].rearrange("p (h c) -> p h c", h=4)
+                if w < 2:
+                    nc.scalar.mul(out=yv, in_=view, mul=Q_SCALE)
+                else:
+                    nc.scalar.copy(out=yv, in_=view)
+                if tau < 12:
+                    if jt == 2:
+                        nc.sync.dma_start(
+                            out=out_t[b, 4 * s : 4 * s + 4, 0:N1, :].rearrange("h (p j) c -> p h (j c)", j=3),
+                            in_=y[:].rearrange("p h j c -> p h (j c)"),
+                        )
+                else:
+                    nc.sync.dma_start(
+                        out=out_t[b, 4 * s : 4 * s + 4, N1:512, :].rearrange("h p c -> p h c"),
+                        in_=y[:],
+                    )
+
+        c32 = const.tile([P, 4, DH], F32, name="c32")
+        s32 = const.tile([P, 4, DH // 2, 2], F32, name="s32")
+        ct1 = const.tile([P, 6 * P], F32, name="ct1")
+        ct2 = const.tile([P, P], F32, name="ct2")
+        st1 = const.tile([P, 6 * P], F32, name="st1")
+        st2 = const.tile([P, P], F32, name="st2")
+        bt32 = [const.tile([P, P], F32, name="bt32%d" % st) for st in range(2)]
+        bcol = [const.tile([P, 16], F32, name="bcol%d" % st) for st in range(2)]
+        spair = strw[:].rearrange("p s (j e) -> p s j e", e=2)
+
+        def set_up(st):
+            nc.gpsimd.tensor_copy(out=bt32[st][:], in_=btile[st][:])
+            pb = ps2p.tile([P, 512], F32, name="ps2", tag="ps2")
+            nc.tensor.transpose(pb[:, 0:P], bt32[st][:], ident[:])
+            nc.scalar.copy(out=bcol[st][:], in_=pb[:, 0:16])
+            lo, hi = (0, 3) if st == 0 else (3, 4)
+            nc.gpsimd.tensor_copy(out=c32[:, lo:hi, :], in_=ctr[:, lo:hi, :])
+            nc.gpsimd.tensor_copy(out=s32[:, lo:hi, :, 0], in_=spair[:, lo:hi, :, 1])
+            nc.gpsimd.tensor_scalar(
+                out=s32[:, lo:hi, :, 1], in0=spair[:, lo:hi, :, 0], scalar1=-1.0, scalar2=0.0, op0=MULT, op1=ADD
+            )
+            for table, long_table, short_table in (
+                (c32[:], ct1, ct2),
+                (s32[:].rearrange("p s j e -> p s (j e)"), st1, st2),
+            ):
+                pt = ps2p.tile([P, 512], F32, name="ps2", tag="ps2")
+                for slot in range(lo, hi):
+                    nc.tensor.transpose(pt[:, P * slot : P * slot + P], table[:, slot, :], ident[:])
+                if st == 0:
+                    nc.scalar.copy(out=long_table[:, 0:384], in_=pt[:, 0:384])
+                    nc.scalar.copy(out=long_table[:, 384:768], in_=pt[:, 0:384])
+                else:
+                    nc.scalar.copy(out=short_table[:], in_=pt[:, 384:512])
 
         w_regroup(0, 0, "v")
         w_regroup(0, 1, "v")
         w_quantise(0)
-        xg0 = x_transposes(0, "ssss")
+        xg0 = x_transposes(0, "sssv")
+        set_up(0)
         x_quantise(0, xg0)
-        pb = ps2p.tile([P, 512], F32, name="ps2", tag="ps2")
-        nc.tensor.transpose(pb[:, 0:P], bt32[:], ident[:])
-        nc.scalar.mul(out=bcol[:, 0:16], in_=pb[:, 0:16], mul=Q_SCALE)
-        nc.scalar.copy(out=bcol[:, 16:32], in_=pb[:, 16:32])
-        xg1 = x_transposes(1, "ssvv")
-        project(0)
+        xg1 = x_transposes(1, "ssss")
+        project(0, range(4))
+        products(0, 0)
+        products(0, 1)
         x_quantise(1, xg1)
+        products(0, 2)
+        products(0, 3)
 
         jobs = [(sl, g) for sl in range(1, 8) for g in range(2)]
+        job_engine = "gsgsgsgsgsgsgs"
         quantise_after = {1: 1, 4: 2, 6: 3, 8: 4, 10: 5, 12: 6, 13: 7}
         xg_late = {}
         for i in range(n_rounds):
-            back_transposes(i)
+            if i == 2:
+                load_w_halves(3)
+                load_w_half(3, 0)
+                load_w_half(3, 1)
+            for half in range(2):
+                if i + 1 < n_rounds:
+                    project(i + 1, (2 * half, 2 * half + 1))
+                    if half == 0:
+                        products(i + 1, 0)
+                finish(i, (2 * half, 2 * half + 1))
             if i == 0:
                 xg_late[0] = (2, x_transposes(2, "ssss"))
-            if i + 1 < n_rounds:
-                project(i + 1)
             if i == 4:
-                cast_tables(3, 4)
+                set_up(1)
             if i == 6:
                 xg_late[7] = (3, x_transposes(3, "ssss"))
             if i < len(jobs):
-                w_regroup(jobs[i][0], jobs[i][1], "s")
-            for tl in range(4):
-                rope(i, tl)
-            if i in xg_late:
-                x_quantise(xg_late[i][0], xg_late[i][1])
+                w_regroup(jobs[i][0], jobs[i][1], job_engine[i])
+            if i + 1 < n_rounds:
+                for hh in range(1, 4):
+                    products(i + 1, hh)
+                    if hh == 1 and i in xg_late:
+                        x_quantise(xg_late[i][0], xg_late[i][1])
             if i in quantise_after:
                 w_quantise(quantise_after[i])

@@ -14,6 +14,7 @@ IDENTITY = mybir.ActivationFunctionType.Identity
 
 P = 128
 D = 1024
+HEADS = 8
 DH = 128
 N1 = 384
 Q_SCALE = DH ** -0.5
@@ -29,6 +30,7 @@ def tile_dualmultiheadattention_pa_kernel(
 ):
     nc = tc.nc
     weights = [wq1, wq2, wk1, wk2]
+    biases = [bq1, bq2, bk1, bk2]
     outs = [out_0, out_0, out_1, out_1]
 
     rounds = []
@@ -45,40 +47,26 @@ def tile_dualmultiheadattention_pa_kernel(
         xgp = ctx.enter_context(tc.tile_pool(name="xgp", bufs=2))
         wgp = ctx.enter_context(tc.tile_pool(name="wgp", bufs=2))
         wcp = ctx.enter_context(tc.tile_pool(name="wcp", bufs=4))
-        abp = ctx.enter_context(tc.tile_pool(name="abp", bufs=8))
-        up = ctx.enter_context(tc.tile_pool(name="up", bufs=2))
+        up = ctx.enter_context(tc.tile_pool(name="up", bufs=8))
+        abp = ctx.enter_context(tc.tile_pool(name="abp", bufs=3))
         y1p = ctx.enter_context(tc.tile_pool(name="y1p", bufs=3))
         y2p = ctx.enter_context(tc.tile_pool(name="y2p", bufs=3))
-        ps1p = ctx.enter_context(tc.psum_pool(name="ps1p", bufs=4))
-        ps2p = ctx.enter_context(tc.psum_pool(name="ps2p", bufs=4))
+        ps1p = ctx.enter_context(tc.psum_pool(name="ps1p", bufs=3))
+        ps2p = ctx.enter_context(tc.psum_pool(name="ps2p", bufs=5))
         if MANUAL:
             ctx.enter_context(tc.manual_schedule())
 
         ident = const.tile([P, P], F32, name="ident")
         masks.make_identity(nc, ident[:])
-        pswap = const.tile([P, P], F32, name="pswap")
-        for e in range(2):
-            nc.gpsimd.tensor_copy(
-                out=pswap[:].rearrange("p (j e) -> p j e", e=2)[:, :, e],
-                in_=ident[:].rearrange("p (j e) -> p j e", e=2)[:, :, 1 - e],
-            )
 
         x1r = [raw.tile([P, 3, D], BF16, name="x1r%d" % b) for b in range(4)]
         x2r = raw.tile([P, 4, D], BF16, name="x2r")
-        whalf = {}
-        wraw = {}
-        for w in (2, 1):
-            wraw[w] = raw.tile([P, 2, 4, D], BF16, name="wraw%d" % w)
+        whalf = [raw.tile([P, 2, 4, 512], BF16, name="whalf%d" % s) for s in range(2)]
+        wraw = [None] + [raw.tile([P, 2, 4, D], BF16, name="wraw%d" % w) for w in range(1, 4)]
 
-        def load_w_halves(w):
-            whalf[w] = []
-            for s in range(2):
-                half_tile = raw.tile([P, 2, 4, 512], BF16, name="whalf%d" % s, tag="whalf%d" % s)
-                whalf[w].append(half_tile)
-
-        def load_w_half(w, s):
-            src = weights[w].rearrange("(m q e) c -> q m e c", m=4, e=2)
-            dst = whalf[w][s][:].rearrange("q g (u e) c -> q (g u) e c", e=2)
+        def load_w_half(s):
+            src = wq1.rearrange("(m q e) c -> q m e c", m=4, e=2)
+            dst = whalf[s][:].rearrange("q g (u e) c -> q (g u) e c", e=2)
             for e in range(2):
                 nc.sync.dma_start(out=dst[:, :, e, :], in_=src[:, :, e, 512 * s : 512 * s + 512])
 
@@ -88,29 +76,41 @@ def tile_dualmultiheadattention_pa_kernel(
                 in_=weights[w].rearrange("(m q e) c -> q m (e c)", m=4, e=2),
             )
 
-        btile = [const.tile([P, P], BF16, name="btile%d" % st) for st in range(2)]
+        btile = const.tile([P, P], BF16, name="btile")
+        nc.vector.memset(btile[:], 0.0)
         ctr = const.tile([P, 4, DH], BF16, name="ctr")
         strw = const.tile([P, 4, DH], BF16, name="strw")
-        for st in range(2):
-            nc.vector.memset(btile[st][:], 0.0)
+        for w in range(4):
+            nc.scalar.dma_start(out=btile[8 * w : 8 * w + 8, :], in_=biases[w].rearrange("(h c) -> h c", c=DH))
         nc.scalar.dma_start(out=ctr[:, 0:3, :], in_=cos1.rearrange("(p j) c -> p j c", j=3))
         nc.scalar.dma_start(out=strw[:, 0:3, :], in_=sin1.rearrange("(p j) c -> p j c", j=3))
-        nc.scalar.dma_start(out=btile[0][0:8, :], in_=bq1.rearrange("(h c) -> h c", c=DH))
-        nc.scalar.dma_start(out=btile[0][8:16, :], in_=bk1.rearrange("(h c) -> h c", c=DH))
-        load_w_halves(0)
-        load_w_half(0, 0)
-        for b in range(2):
+        load_w_half(0)
+        for b in range(4):
             nc.sync.dma_start(out=x1r[b][:], in_=x_1[b].rearrange("(p j) k -> p j k", j=3))
-        for b in range(2, 4):
-            nc.sync.dma_start(out=x1r[b][:], in_=x_1[b].rearrange("(p j) k -> p j k", j=3))
-        load_w_half(0, 1)
+        load_w_half(1)
         load_w_full(2)
         nc.sync.dma_start(out=x2r[:], in_=x_2.rearrange("b p k -> p b k"))
         nc.sync.dma_start(out=ctr[:, 3, :], in_=cos2)
         nc.sync.dma_start(out=strw[:, 3, :], in_=sin2)
-        nc.sync.dma_start(out=btile[1][0:8, :], in_=bq2.rearrange("(h c) -> h c", c=DH))
-        nc.sync.dma_start(out=btile[1][8:16, :], in_=bk2.rearrange("(h c) -> h c", c=DH))
         load_w_full(1)
+        load_w_full(3)
+
+        bt32 = const.tile([P, P], F32, name="bt32")
+        bcol = const.tile([P, 32], F32, name="bcol")
+        ctab = const.tile([P, 4, DH], F32, name="ctab")
+        stab = const.tile([P, 4, DH], F32, name="stab")
+        spair = strw[:].rearrange("p s (j e) -> p s j e", e=2)
+        stab_pair = stab[:].rearrange("p s (j e) -> p s j e", e=2)
+        nc.gpsimd.tensor_copy(out=bt32[:], in_=btile[:])
+
+        def cast_tables(lo, hi):
+            nc.gpsimd.tensor_copy(out=ctab[:, lo:hi, :], in_=ctr[:, lo:hi, :])
+            nc.gpsimd.tensor_scalar(
+                out=stab_pair[:, lo:hi, :, 0], in0=spair[:, lo:hi, :, 0], scalar1=-1.0, scalar2=0.0, op0=MULT, op1=ADD
+            )
+            nc.gpsimd.tensor_copy(out=stab_pair[:, lo:hi, :, 1], in_=spair[:, lo:hi, :, 1])
+
+        cast_tables(0, 3)
 
         xc = [const.tile([P, 2, 512], U32, name="xc%d" % g, align_bytes=64) for g in range(4)]
         xs = [const.tile([P, 2, 512], U8, name="xs%d" % g, align_bytes=64) for g in range(4)]
@@ -124,7 +124,7 @@ def tile_dualmultiheadattention_pa_kernel(
                     src = x1r[tau // 3][:, tau % 3, :].bitcast(F32)
                 else:
                     src = x2r[:, tau - 12, :].bitcast(F32)
-                xt = ps2p.tile([P, 512], F32, name="ps2", tag="ps2")
+                xt = ps1p.tile([P, 512], F32, name="ps1", tag="ps1")
                 for m in range(4):
                     nc.tensor.transpose(xt[:, P * m : P * m + P], src[:, P * m : P * m + P], ident[:])
                 dst = xg32[:, :, P * tl : P * tl + P, :]
@@ -136,12 +136,11 @@ def tile_dualmultiheadattention_pa_kernel(
             return xg
 
         def x_quantise(grp, xg):
-            for g in range(2):
-                nc.vector.quantize_mx(
-                    out=xc[grp][:, g, :].bitcast(FP8X4),
-                    scales=xs[grp][:, g, :],
-                    in_=xg[:, g, :, :].rearrange("p t k -> p (t k)"),
-                )
+            nc.vector.quantize_mx(
+                out=xc[grp][:].rearrange("p g t -> p (g t)").bitcast(FP8X4),
+                scales=xs[grp][:].rearrange("p g t -> p (g t)"),
+                in_=xg[:].rearrange("p g t k -> p (g t k)"),
+            )
 
         wg_tiles = {}
         w_codes = {}
@@ -150,22 +149,16 @@ def tile_dualmultiheadattention_pa_kernel(
             w, s = SLICES[sl]
             if g == 0:
                 wg_tiles[sl] = wgp.tile([P, 2, 512, 4], BF16, name="wg", tag="wg", align_bytes=64)
-            if w in whalf:
-                rows = whalf[w][s][:, g, :, :]
+            if w == 0:
+                rows = whalf[s][:, g, :, :]
             else:
                 rows = wraw[w][:, g, :, 512 * s : 512 * s + 512]
             src = rows.rearrange("p t (c i) -> p c t i", i=4)
             dst = wg_tiles[sl][:, g, :, :].rearrange("p (c i) t -> p c t i", i=4)
             if engine == "s":
                 nc.scalar.copy(out=dst, in_=src)
-            elif engine == "v":
-                nc.vector.tensor_copy(out=dst, in_=src)
             else:
-                nc.gpsimd.tensor_scalar(
-                    out=wg_tiles[sl][:, g, :, :],
-                    in0=rows.rearrange("p t c -> p c t"),
-                    scalar1=1.0, scalar2=0.0, op0=MULT, op1=ADD,
-                )
+                nc.vector.tensor_copy(out=dst, in_=src)
 
         def w_quantise(sl):
             wc = wcp.tile([P, 2, 512], U32, name="wc", tag="wc", align_bytes=64)
@@ -177,17 +170,15 @@ def tile_dualmultiheadattention_pa_kernel(
             )
             w_codes[sl] = (wc, ws)
 
-        ps1_tiles = {}
-        ab_tiles = {}
+        u_tiles = {}
 
-        def project(r, heads):
+        def project(r):
             sl, grp = rounds[r]
+            w, s = SLICES[sl]
             wc, ws = w_codes[sl]
-            if r not in ps1_tiles:
-                ps1_tiles[r] = []
-                ab_tiles[r] = []
-            banks = ps1_tiles[r]
-            for hh in heads:
+            scale = Q_SCALE if w < 2 else 1.0
+            us = []
+            for hh in range(4):
                 ps = ps1p.tile([P, 512], F32, name="ps1", tag="ps1")
                 for g in range(2):
                     nc.tensor.matmul_mx(
@@ -199,172 +190,101 @@ def tile_dualmultiheadattention_pa_kernel(
                         start=(g == 0),
                         stop=(g == 1),
                     )
-                banks.append(ps)
-
-        def products(r, hh):
-            sl, grp = rounds[r]
-            w, s = SLICES[sl]
-            bias = bcol[w % 2][:, 8 * (w // 2) + 4 * s + hh : 8 * (w // 2) + 4 * s + hh + 1]
-            ps = ps1_tiles[r][hh]
-            pair = []
-            if hh == 0:
                 u = up.tile([P, 512], F32, name="u", tag="u")
-                nc.scalar.activation(out=u[:], in_=ps[:], func=IDENTITY, bias=bias, scale=1.0)
-                for name, long_table, short_table in (("a", ct1, ct2), ("b", st1, st2)):
-                    t = abp.tile([P, 512], F32, name=name, tag=name)
-                    if grp < 3:
-                        nc.gpsimd.tensor_tensor(
-                            out=t[:], in0=u[:], in1=long_table[:, P * grp : P * grp + 512], op=MULT
-                        )
-                    else:
-                        nc.gpsimd.tensor_tensor(
-                            out=t[:].rearrange("p (t n) -> p t n", t=4),
-                            in0=u[:].rearrange("p (t n) -> p t n", t=4),
-                            in1=short_table[:].unsqueeze(1).to_broadcast([P, 4, P]),
-                            op=MULT,
-                        )
-                    pair.append(t)
-                ab_tiles[r].append(pair)
-                return
-            for name, long_table, short_table in (("a", ct1, ct2), ("b", st1, st2)):
-                t = abp.tile([P, 512], F32, name=name, tag=name)
-                if grp < 3:
-                    nc.vector.scalar_tensor_tensor(
-                        out=t[:], in0=ps[:], scalar=bias,
-                        in1=long_table[:, P * grp : P * grp + 512], op0=ADD, op1=MULT,
-                    )
-                else:
-                    nc.vector.scalar_tensor_tensor(
-                        out=t[:].rearrange("p (t n) -> p t n", t=4),
-                        in0=ps[:].rearrange("p (t n) -> p t n", t=4),
-                        scalar=bias,
-                        in1=short_table[:].unsqueeze(1).to_broadcast([P, 4, P]),
-                        op0=ADD, op1=MULT,
-                    )
-                pair.append(t)
-            ab_tiles[r].append(pair)
+                col = 8 * w + 4 * s + hh
+                nc.scalar.activation(out=u[:], in_=ps[:], func=IDENTITY, bias=bcol[:, col : col + 1], scale=scale)
+                us.append(u)
+            u_tiles[r] = us
 
         y_open = {}
+        ps2_tiles = {}
 
-        def finish(r, tiles):
+        def back_transposes(r):
+            us = u_tiles[r]
+            banks = []
+            for tl in range(4):
+                ps2 = ps2p.tile([P, 512], F32, name="ps2", tag="ps2")
+                for hh in range(4):
+                    nc.tensor.transpose(ps2[:, P * hh : P * hh + P], us[hh][:, P * tl : P * tl + P], ident[:])
+                banks.append(ps2)
+            ps2_tiles[r] = banks
+
+        def rope(r, tl):
             sl, grp = rounds[r]
             w, s = SLICES[sl]
             out_t = outs[w]
-            for tl in tiles:
-                tau = 4 * grp + tl
-                ps2 = ps2p.tile([P, 512], F32, name="ps2", tag="ps2")
-                for hh in range(4):
-                    a, b2 = ab_tiles[r][hh]
-                    nc.tensor.matmul(
-                        out=ps2[:, P * hh : P * hh + P], lhsT=a[:, P * tl : P * tl + P], rhs=ident[:],
-                        start=True, stop=False, is_transpose=True,
-                    )
-                    nc.tensor.matmul(
-                        out=ps2[:, P * hh : P * hh + P], lhsT=b2[:, P * tl : P * tl + P], rhs=pswap[:],
-                        start=False, stop=True, is_transpose=True,
-                    )
-                if tau < 12:
-                    b, jt = tau // 3, tau % 3
-                    if jt == 0:
-                        y_open[b] = y1p.tile([P, 4, 3, DH], F32, name="y1", tag="y1")
-                    y = y_open[b]
-                    yv = y[:, :, jt, :]
-                else:
-                    b, jt = tau - 12, 0
-                    y = y2p.tile([P, 4, DH], F32, name="y2", tag="y2")
-                    yv = y[:]
-                view = ps2[:].rearrange("p (h c) -> p h c", h=4)
-                if w < 2:
-                    nc.scalar.mul(out=yv, in_=view, mul=Q_SCALE)
-                else:
-                    nc.scalar.copy(out=yv, in_=view)
-                if tau < 12:
-                    if jt == 2:
-                        nc.sync.dma_start(
-                            out=out_t[b, 4 * s : 4 * s + 4, 0:N1, :].rearrange("h (p j) c -> p h (j c)", j=3),
-                            in_=y[:].rearrange("p h j c -> p h (j c)"),
-                        )
-                else:
-                    nc.sync.dma_start(
-                        out=out_t[b, 4 * s : 4 * s + 4, N1:512, :].rearrange("h p c -> p h c"),
-                        in_=y[:],
-                    )
-
-        c32 = const.tile([P, 4, DH], F32, name="c32")
-        s32 = const.tile([P, 4, DH // 2, 2], F32, name="s32")
-        ct1 = const.tile([P, 6 * P], F32, name="ct1")
-        ct2 = const.tile([P, P], F32, name="ct2")
-        st1 = const.tile([P, 6 * P], F32, name="st1")
-        st2 = const.tile([P, P], F32, name="st2")
-        bt32 = [const.tile([P, P], F32, name="bt32%d" % st) for st in range(2)]
-        bcol = [const.tile([P, 16], F32, name="bcol%d" % st) for st in range(2)]
-        spair = strw[:].rearrange("p s (j e) -> p s j e", e=2)
-
-        def set_up(st):
-            nc.gpsimd.tensor_copy(out=bt32[st][:], in_=btile[st][:])
-            pb = ps2p.tile([P, 512], F32, name="ps2", tag="ps2")
-            nc.tensor.transpose(pb[:, 0:P], bt32[st][:], ident[:])
-            nc.scalar.copy(out=bcol[st][:], in_=pb[:, 0:16])
-            lo, hi = (0, 3) if st == 0 else (3, 4)
-            nc.gpsimd.tensor_copy(out=c32[:, lo:hi, :], in_=ctr[:, lo:hi, :])
-            nc.gpsimd.tensor_copy(out=s32[:, lo:hi, :, 0], in_=spair[:, lo:hi, :, 1])
-            nc.gpsimd.tensor_scalar(
-                out=s32[:, lo:hi, :, 1], in0=spair[:, lo:hi, :, 0], scalar1=-1.0, scalar2=0.0, op0=MULT, op1=ADD
+            tau = 4 * grp + tl
+            ps2 = ps2_tiles[r][tl]
+            slot = tau % 3 if tau < 12 else 3
+            a = abp.tile([P, 4, DH], F32, name="a", tag="a")
+            nc.vector.tensor_tensor(
+                out=a[:],
+                in0=ps2[:].rearrange("p (h c) -> p h c", h=4),
+                in1=ctab[:, slot, :].unsqueeze(1).to_broadcast([P, 4, DH]),
+                op=MULT,
             )
-            for table, long_table, short_table in (
-                (c32[:], ct1, ct2),
-                (s32[:].rearrange("p s j e -> p s (j e)"), st1, st2),
-            ):
-                pt = ps2p.tile([P, 512], F32, name="ps2", tag="ps2")
-                for slot in range(lo, hi):
-                    nc.tensor.transpose(pt[:, P * slot : P * slot + P], table[:, slot, :], ident[:])
-                if st == 0:
-                    nc.scalar.copy(out=long_table[:, 0:384], in_=pt[:, 0:384])
-                    nc.scalar.copy(out=long_table[:, 384:768], in_=pt[:, 0:384])
-                else:
-                    nc.scalar.copy(out=short_table[:], in_=pt[:, 384:512])
+            bt = abp.tile([P, 4, DH], F32, name="bt", tag="bt")
+            crossed = ps2[:].rearrange("p (h j e) -> p h j e", h=4, e=2)[:, :, :, ::-1]
+            nc.vector.tensor_tensor(
+                out=bt[:].rearrange("p h (j e) -> p h j e", e=2),
+                in0=crossed,
+                in1=stab_pair[:, slot, :, :].unsqueeze(1).to_broadcast([P, 4, DH // 2, 2]),
+                op=MULT,
+            )
+            if tau < 12:
+                b, jt = tau // 3, tau % 3
+                if jt == 0:
+                    y_open[b] = y1p.tile([P, 4, 3, DH], F32, name="y1", tag="y1")
+                y = y_open[b]
+                yv = y[:, :, jt, :]
+            else:
+                b, jt = tau - 12, 0
+                y = y2p.tile([P, 4, DH], F32, name="y2", tag="y2")
+                yv = y[:]
+            nc.gpsimd.tensor_tensor(out=yv, in0=a[:], in1=bt[:], op=ADD)
+            if tau < 12:
+                if jt == 2:
+                    nc.sync.dma_start(
+                        out=out_t[b, 4 * s : 4 * s + 4, 0:N1, :].rearrange("h (p j) c -> p h (j c)", j=3),
+                        in_=y[:].rearrange("p h j c -> p h (j c)"),
+                    )
+            else:
+                nc.sync.dma_start(
+                    out=out_t[b, 4 * s : 4 * s + 4, N1:512, :].rearrange("h p c -> p h c"),
+                    in_=y[:],
+                )
 
         w_regroup(0, 0, "v")
         w_regroup(0, 1, "v")
         w_quantise(0)
-        xg0 = x_transposes(0, "sssv")
-        set_up(0)
+        xg0 = x_transposes(0, "ssss")
         x_quantise(0, xg0)
-        xg1 = x_transposes(1, "ssss")
-        project(0, range(4))
-        products(0, 0)
-        products(0, 1)
+        pb = ps2p.tile([P, 512], F32, name="ps2", tag="ps2")
+        nc.tensor.transpose(pb[:, 0:P], bt32[:], ident[:])
+        nc.scalar.mul(out=bcol[:, 0:16], in_=pb[:, 0:16], mul=Q_SCALE)
+        nc.scalar.copy(out=bcol[:, 16:32], in_=pb[:, 16:32])
+        xg1 = x_transposes(1, "ssvv")
+        project(0)
         x_quantise(1, xg1)
-        products(0, 2)
-        products(0, 3)
 
         jobs = [(sl, g) for sl in range(1, 8) for g in range(2)]
-        job_engine = "gsgsgsgsgsgsgs"
         quantise_after = {1: 1, 4: 2, 6: 3, 8: 4, 10: 5, 12: 6, 13: 7}
         xg_late = {}
         for i in range(n_rounds):
-            if i == 2:
-                load_w_halves(3)
-                load_w_half(3, 0)
-                load_w_half(3, 1)
-            for half in range(2):
-                if i + 1 < n_rounds:
-                    project(i + 1, (2 * half, 2 * half + 1))
-                    if half == 0:
-                        products(i + 1, 0)
-                finish(i, (2 * half, 2 * half + 1))
+            back_transposes(i)
             if i == 0:
                 xg_late[0] = (2, x_transposes(2, "ssss"))
+            if i + 1 < n_rounds:
+                project(i + 1)
             if i == 4:
-                set_up(1)
+                cast_tables(3, 4)
             if i == 6:
                 xg_late[7] = (3, x_transposes(3, "ssss"))
             if i < len(jobs):
-                w_regroup(jobs[i][0], jobs[i][1], job_engine[i])
-            if i + 1 < n_rounds:
-                for hh in range(1, 4):
-                    products(i + 1, hh)
-                    if hh == 1 and i in xg_late:
-                        x_quantise(xg_late[i][0], xg_late[i][1])
+                w_regroup(jobs[i][0], jobs[i][1], "s")
+            for tl in range(4):
+                rope(i, tl)
+            if i in xg_late:
+                x_quantise(xg_late[i][0], xg_late[i][1])
             if i in quantise_after:
                 w_quantise(quantise_after[i])

@@ -14,277 +14,237 @@ IDENTITY = mybir.ActivationFunctionType.Identity
 
 P = 128
 D = 1024
-HEADS = 8
-DH = 128
+PASSES = 2
+WIDE = 512
 N1 = 384
-Q_SCALE = DH ** -0.5
+Q_SCALE = P ** -0.5
 FLOPS = 2 * 2048 * 1024 * 2048
-
-MANUAL = True
-
-SLICES = [(0, 0), (0, 1), (2, 0), (2, 1), (1, 0), (1, 1), (3, 0), (3, 1)]
 
 
 def tile_dualmultiheadattention_pa_kernel(
     tc, x_1, x_2, cos1, sin1, cos2, sin2, wq1, bq1, wk1, bk1, wq2, bq2, wk2, bk2, out_0, out_1
 ):
     nc = tc.nc
-    weights = [wq1, wq2, wk1, wk2]
-    biases = [bq1, bq2, bk1, bk2]
-    outs = [out_0, out_0, out_1, out_1]
-
-    rounds = []
-    for sl in range(8):
-        if SLICES[sl][0] in (0, 2):
-            rounds.extend([(sl, 0), (sl, 1), (sl, 2)])
-        else:
-            rounds.append((sl, 3))
+    projections = [
+        (wq1, bq1, out_0, Q_SCALE, (0, 1, 2)),
+        (wk1, bk1, out_1, 1.0, (0, 1, 2)),
+        (wq2, bq2, out_0, Q_SCALE, (3,)),
+        (wk2, bk2, out_1, 1.0, (3,)),
+    ]
+    rounds = [(sl, grp) for sl in range(8) for grp in projections[sl // 2][4]]
     n_rounds = len(rounds)
 
     with ExitStack() as ctx:
         const = ctx.enter_context(tc.tile_pool(name="const", bufs=1))
         raw = ctx.enter_context(tc.tile_pool(name="raw", bufs=1))
-        xgp = ctx.enter_context(tc.tile_pool(name="xgp", bufs=2))
-        wgp = ctx.enter_context(tc.tile_pool(name="wgp", bufs=2))
-        wcp = ctx.enter_context(tc.tile_pool(name="wcp", bufs=4))
-        up = ctx.enter_context(tc.tile_pool(name="up", bufs=8))
-        abp = ctx.enter_context(tc.tile_pool(name="abp", bufs=3))
-        y1p = ctx.enter_context(tc.tile_pool(name="y1p", bufs=3))
-        y2p = ctx.enter_context(tc.tile_pool(name="y2p", bufs=3))
-        ps1p = ctx.enter_context(tc.psum_pool(name="ps1p", bufs=3))
-        ps2p = ctx.enter_context(tc.psum_pool(name="ps2p", bufs=5))
-        if MANUAL:
-            ctx.enter_context(tc.manual_schedule())
+        x_grouped_pool = ctx.enter_context(tc.tile_pool(name="x_grouped", bufs=2))
+        w_grouped_pool = ctx.enter_context(tc.tile_pool(name="w_grouped", bufs=2))
+        w_codes_pool = ctx.enter_context(tc.tile_pool(name="w_codes", bufs=4))
+        biased_pool = ctx.enter_context(tc.tile_pool(name="biased", bufs=8))
+        products_pool = ctx.enter_context(tc.tile_pool(name="products", bufs=3))
+        y1_pool = ctx.enter_context(tc.tile_pool(name="y1", bufs=3))
+        y2_pool = ctx.enter_context(tc.tile_pool(name="y2", bufs=3))
+        mx_banks = ctx.enter_context(tc.psum_pool(name="mx_banks", bufs=3))
+        back_banks = ctx.enter_context(tc.psum_pool(name="back_banks", bufs=5))
+        ctx.enter_context(tc.manual_schedule())
 
         ident = const.tile([P, P], F32, name="ident")
         masks.make_identity(nc, ident[:])
 
-        x1r = [raw.tile([P, 3, D], BF16, name="x1r%d" % b) for b in range(4)]
-        x2r = raw.tile([P, 4, D], BF16, name="x2r")
-        whalf = [raw.tile([P, 2, 4, 512], BF16, name="whalf%d" % s) for s in range(2)]
-        wraw = [None] + [raw.tile([P, 2, 4, D], BF16, name="wraw%d" % w) for w in range(1, 4)]
-
-        def load_w_half(s):
-            src = wq1.rearrange("(m q e) c -> q m e c", m=4, e=2)
-            dst = whalf[s][:].rearrange("q g (u e) c -> q (g u) e c", e=2)
-            for e in range(2):
-                nc.sync.dma_start(out=dst[:, :, e, :], in_=src[:, :, e, 512 * s : 512 * s + 512])
-
-        def load_w_full(w):
-            nc.sync.dma_start(
-                out=wraw[w][:].rearrange("q g (u e) c -> q (g u) (e c)", e=2),
-                in_=weights[w].rearrange("(m q e) c -> q m (e c)", m=4, e=2),
-            )
-
-        btile = const.tile([P, P], BF16, name="btile")
-        nc.vector.memset(btile[:], 0.0)
-        ctr = const.tile([P, 4, DH], BF16, name="ctr")
-        strw = const.tile([P, 4, DH], BF16, name="strw")
+        bias_rows = const.tile([P, P], BF16, name="bias_rows")
+        nc.vector.memset(bias_rows[:], 0.0)
         for w in range(4):
-            nc.scalar.dma_start(out=btile[8 * w : 8 * w + 8, :], in_=biases[w].rearrange("(h c) -> h c", c=DH))
-        nc.scalar.dma_start(out=ctr[:, 0:3, :], in_=cos1.rearrange("(p j) c -> p j c", j=3))
-        nc.scalar.dma_start(out=strw[:, 0:3, :], in_=sin1.rearrange("(p j) c -> p j c", j=3))
-        load_w_half(0)
+            nc.scalar.dma_start(
+                out=bias_rows[8 * w : 8 * w + 8, :], in_=projections[w][1].rearrange("(h c) -> h c", c=P)
+            )
+        cos_bf = const.tile([P, 4, P], BF16, name="cos_bf")
+        sin_bf = const.tile([P, 4, P], BF16, name="sin_bf")
+        nc.scalar.dma_start(out=cos_bf[:, 0:3, :], in_=cos1.rearrange("(p j) c -> p j c", j=3))
+        nc.scalar.dma_start(out=sin_bf[:, 0:3, :], in_=sin1.rearrange("(p j) c -> p j c", j=3))
+        nc.scalar.dma_start(out=cos_bf[:, 3, :], in_=cos2)
+        nc.scalar.dma_start(out=sin_bf[:, 3, :], in_=sin2)
+
+        w_raw = [raw.tile([P, PASSES, 4, WIDE], BF16, name="w_raw%d" % sl) for sl in range(8)]
+
+        def load_slice(sl):
+            rows = projections[sl // 2][0].rearrange("(m q e) c -> q m e c", m=2 * PASSES, e=2)
+            dst = w_raw[sl][:].rearrange("q g (u e) c -> q (g u) e c", e=2)
+            first = WIDE * (sl % 2)
+            for e in range(2):
+                nc.sync.dma_start(out=dst[:, :, e, :], in_=rows[:, :, e, first : first + WIDE])
+
+        x1_raw = [raw.tile([P, 3, D], BF16, name="x1_raw%d" % b) for b in range(4)]
+        x2_raw = raw.tile([P, 4, D], BF16, name="x2_raw")
+        load_slice(0)
         for b in range(4):
-            nc.sync.dma_start(out=x1r[b][:], in_=x_1[b].rearrange("(p j) k -> p j k", j=3))
-        load_w_half(1)
-        load_w_full(2)
-        nc.sync.dma_start(out=x2r[:], in_=x_2.rearrange("b p k -> p b k"))
-        nc.sync.dma_start(out=ctr[:, 3, :], in_=cos2)
-        nc.sync.dma_start(out=strw[:, 3, :], in_=sin2)
-        load_w_full(1)
-        load_w_full(3)
+            nc.sync.dma_start(out=x1_raw[b][:], in_=x_1[b].rearrange("(p j) k -> p j k", j=3))
+        load_slice(1)
+        nc.sync.dma_start(out=x2_raw[:], in_=x_2.rearrange("b p k -> p b k"))
+        for sl in range(2, 8):
+            load_slice(sl)
 
-        bt32 = const.tile([P, P], F32, name="bt32")
-        bcol = const.tile([P, 32], F32, name="bcol")
-        ctab = const.tile([P, 4, DH], F32, name="ctab")
-        stab = const.tile([P, 4, DH], F32, name="stab")
-        spair = strw[:].rearrange("p s (j e) -> p s j e", e=2)
-        stab_pair = stab[:].rearrange("p s (j e) -> p s j e", e=2)
-        nc.gpsimd.tensor_copy(out=bt32[:], in_=btile[:])
+        bias_f32 = const.tile([P, P], F32, name="bias_f32")
+        nc.gpsimd.tensor_copy(out=bias_f32[:], in_=bias_rows[:])
+        cos_tab = const.tile([P, 4, P], F32, name="cos_tab")
+        nc.gpsimd.tensor_copy(out=cos_tab[:], in_=cos_bf[:])
+        sin_tab = const.tile([P, 4, P], F32, name="sin_tab")
+        sin_bf_pairs = sin_bf[:].rearrange("p s (j e) -> p s j e", e=2)
+        sin_pairs = sin_tab[:].rearrange("p s (j e) -> p s j e", e=2)
+        nc.gpsimd.tensor_scalar(
+            out=sin_pairs[:, :, :, 0], in0=sin_bf_pairs[:, :, :, 0], scalar1=-1.0, scalar2=0.0, op0=MULT, op1=ADD
+        )
+        nc.gpsimd.tensor_copy(out=sin_pairs[:, :, :, 1], in_=sin_bf_pairs[:, :, :, 1])
 
-        def cast_tables(lo, hi):
-            nc.gpsimd.tensor_copy(out=ctab[:, lo:hi, :], in_=ctr[:, lo:hi, :])
-            nc.gpsimd.tensor_scalar(
-                out=stab_pair[:, lo:hi, :, 0], in0=spair[:, lo:hi, :, 0], scalar1=-1.0, scalar2=0.0, op0=MULT, op1=ADD
-            )
-            nc.gpsimd.tensor_copy(out=stab_pair[:, lo:hi, :, 1], in_=spair[:, lo:hi, :, 1])
+        x_codes = [const.tile([P, PASSES, WIDE], U32, name="x_codes%d" % g, align_bytes=64) for g in range(4)]
+        x_scales = [const.tile([P, PASSES, WIDE], U8, name="x_scales%d" % g, align_bytes=64) for g in range(4)]
+        x_grouped = {}
 
-        cast_tables(0, 3)
-
-        xc = [const.tile([P, 2, 512], U32, name="xc%d" % g, align_bytes=64) for g in range(4)]
-        xs = [const.tile([P, 2, 512], U8, name="xs%d" % g, align_bytes=64) for g in range(4)]
-
-        def x_transposes(grp, engines):
-            xg = xgp.tile([P, 2, 512, 4], BF16, name="xg", tag="xg", align_bytes=64)
-            xg32 = xg[:].bitcast(F32)
+        def transpose_x(grp, copy):
+            x_grouped[grp] = x_grouped_pool.tile([P, PASSES, WIDE, 4], BF16, name="x_grouped", align_bytes=64)
+            words = x_grouped[grp][:].bitcast(F32)
             for tl in range(4):
-                tau = 4 * grp + tl
-                if tau < 12:
-                    src = x1r[tau // 3][:, tau % 3, :].bitcast(F32)
+                tile_no = 4 * grp + tl
+                if grp < 3:
+                    tokens = x1_raw[tile_no // 3][:, tile_no % 3, :].bitcast(F32)
                 else:
-                    src = x2r[:, tau - 12, :].bitcast(F32)
-                xt = ps1p.tile([P, 512], F32, name="ps1", tag="ps1")
-                for m in range(4):
-                    nc.tensor.transpose(xt[:, P * m : P * m + P], src[:, P * m : P * m + P], ident[:])
-                dst = xg32[:, :, P * tl : P * tl + P, :]
-                view = xt[:].rearrange("p (g u t) -> p g t u", g=2, u=2)
-                if engines[tl] == "s":
-                    nc.scalar.copy(out=dst, in_=view)
-                else:
-                    nc.vector.tensor_copy(out=dst, in_=view)
-            return xg
+                    tokens = x2_raw[:, tl, :].bitcast(F32)
+                bank = mx_banks.tile([P, WIDE], F32, name="mx_bank")
+                for m in range(2 * PASSES):
+                    nc.tensor.transpose(bank[:, P * m : P * m + P], tokens[:, P * m : P * m + P], ident[:])
+                copy(
+                    out=words[:, :, P * tl : P * tl + P, :],
+                    in_=bank[:].rearrange("p (g u t) -> p g t u", g=PASSES, u=2),
+                )
 
-        def x_quantise(grp, xg):
+        def quantise_x(grp):
             nc.vector.quantize_mx(
-                out=xc[grp][:].rearrange("p g t -> p (g t)").bitcast(FP8X4),
-                scales=xs[grp][:].rearrange("p g t -> p (g t)"),
-                in_=xg[:].rearrange("p g t k -> p (g t k)"),
+                out=x_codes[grp][:].rearrange("p g t -> p (g t)").bitcast(FP8X4),
+                scales=x_scales[grp][:].rearrange("p g t -> p (g t)"),
+                in_=x_grouped[grp][:].rearrange("p g t k -> p (g t k)"),
             )
 
-        wg_tiles = {}
+        w_grouped = {}
         w_codes = {}
 
-        def w_regroup(sl, g, engine):
-            w, s = SLICES[sl]
+        def regroup_w(sl, g, copy):
             if g == 0:
-                wg_tiles[sl] = wgp.tile([P, 2, 512, 4], BF16, name="wg", tag="wg", align_bytes=64)
-            if w == 0:
-                rows = whalf[s][:, g, :, :]
-            else:
-                rows = wraw[w][:, g, :, 512 * s : 512 * s + 512]
-            src = rows.rearrange("p t (c i) -> p c t i", i=4)
-            dst = wg_tiles[sl][:, g, :, :].rearrange("p (c i) t -> p c t i", i=4)
-            if engine == "s":
-                nc.scalar.copy(out=dst, in_=src)
-            else:
-                nc.vector.tensor_copy(out=dst, in_=src)
-
-        def w_quantise(sl):
-            wc = wcp.tile([P, 2, 512], U32, name="wc", tag="wc", align_bytes=64)
-            ws = wcp.tile([P, 2, 512], U8, name="ws", tag="ws", align_bytes=64)
-            nc.vector.quantize_mx(
-                out=wc[:].rearrange("p g c -> p (g c)").bitcast(FP8X4),
-                scales=ws[:].rearrange("p g c -> p (g c)"),
-                in_=wg_tiles[sl][:].rearrange("p g c t -> p (g c t)"),
+                w_grouped[sl] = w_grouped_pool.tile([P, PASSES, WIDE, 4], BF16, name="w_grouped", align_bytes=64)
+            copy(
+                out=w_grouped[sl][:, g, :, :].rearrange("p (c i) t -> p c t i", i=4),
+                in_=w_raw[sl][:, g, :, :].rearrange("p t (c i) -> p c t i", i=4),
             )
-            w_codes[sl] = (wc, ws)
 
-        u_tiles = {}
+        def quantise_w(sl):
+            codes = w_codes_pool.tile([P, PASSES, WIDE], U32, name="w_code_words", align_bytes=64)
+            scales = w_codes_pool.tile([P, PASSES, WIDE], U8, name="w_scales", align_bytes=64)
+            nc.vector.quantize_mx(
+                out=codes[:].rearrange("p g c -> p (g c)").bitcast(FP8X4),
+                scales=scales[:].rearrange("p g c -> p (g c)"),
+                in_=w_grouped[sl][:].rearrange("p g c t -> p (g c t)"),
+            )
+            w_codes[sl] = (codes, scales)
+
+        bias_cols = const.tile([P, 32], F32, name="bias_cols")
+        biased = {}
 
         def project(r):
             sl, grp = rounds[r]
-            w, s = SLICES[sl]
-            wc, ws = w_codes[sl]
-            scale = Q_SCALE if w < 2 else 1.0
-            us = []
+            codes, scales = w_codes[sl]
+            biased[r] = []
             for hh in range(4):
-                ps = ps1p.tile([P, 512], F32, name="ps1", tag="ps1")
-                for g in range(2):
+                bank = mx_banks.tile([P, WIDE], F32, name="mx_bank")
+                for g in range(PASSES):
                     nc.tensor.matmul_mx(
-                        out=ps[:],
-                        lhsT=wc[:, g, P * hh : P * hh + P].bitcast(FP8X4),
-                        lhsT_scale=ws[:, g, P * hh : P * hh + P],
-                        rhs=xc[grp][:, g, :].bitcast(FP8X4),
-                        rhs_scale=xs[grp][:, g, :],
+                        out=bank[:],
+                        lhsT=codes[:, g, P * hh : P * hh + P].bitcast(FP8X4),
+                        lhsT_scale=scales[:, g, P * hh : P * hh + P],
+                        rhs=x_codes[grp][:, g, :].bitcast(FP8X4),
+                        rhs_scale=x_scales[grp][:, g, :],
                         start=(g == 0),
-                        stop=(g == 1),
+                        stop=(g == PASSES - 1),
                     )
-                u = up.tile([P, 512], F32, name="u", tag="u")
-                col = 8 * w + 4 * s + hh
-                nc.scalar.activation(out=u[:], in_=ps[:], func=IDENTITY, bias=bcol[:, col : col + 1], scale=scale)
-                us.append(u)
-            u_tiles[r] = us
-
-        y_open = {}
-        ps2_tiles = {}
-
-        def back_transposes(r):
-            us = u_tiles[r]
-            banks = []
-            for tl in range(4):
-                ps2 = ps2p.tile([P, 512], F32, name="ps2", tag="ps2")
-                for hh in range(4):
-                    nc.tensor.transpose(ps2[:, P * hh : P * hh + P], us[hh][:, P * tl : P * tl + P], ident[:])
-                banks.append(ps2)
-            ps2_tiles[r] = banks
-
-        def rope(r, tl):
-            sl, grp = rounds[r]
-            w, s = SLICES[sl]
-            out_t = outs[w]
-            tau = 4 * grp + tl
-            ps2 = ps2_tiles[r][tl]
-            slot = tau % 3 if tau < 12 else 3
-            a = abp.tile([P, 4, DH], F32, name="a", tag="a")
-            nc.vector.tensor_tensor(
-                out=a[:],
-                in0=ps2[:].rearrange("p (h c) -> p h c", h=4),
-                in1=ctab[:, slot, :].unsqueeze(1).to_broadcast([P, 4, DH]),
-                op=MULT,
-            )
-            bt = abp.tile([P, 4, DH], F32, name="bt", tag="bt")
-            crossed = ps2[:].rearrange("p (h j e) -> p h j e", h=4, e=2)[:, :, :, ::-1]
-            nc.vector.tensor_tensor(
-                out=bt[:].rearrange("p h (j e) -> p h j e", e=2),
-                in0=crossed,
-                in1=stab_pair[:, slot, :, :].unsqueeze(1).to_broadcast([P, 4, DH // 2, 2]),
-                op=MULT,
-            )
-            if tau < 12:
-                b, jt = tau // 3, tau % 3
-                if jt == 0:
-                    y_open[b] = y1p.tile([P, 4, 3, DH], F32, name="y1", tag="y1")
-                y = y_open[b]
-                yv = y[:, :, jt, :]
-            else:
-                b, jt = tau - 12, 0
-                y = y2p.tile([P, 4, DH], F32, name="y2", tag="y2")
-                yv = y[:]
-            nc.gpsimd.tensor_tensor(out=yv, in0=a[:], in1=bt[:], op=ADD)
-            if tau < 12:
-                if jt == 2:
-                    nc.sync.dma_start(
-                        out=out_t[b, 4 * s : 4 * s + 4, 0:N1, :].rearrange("h (p j) c -> p h (j c)", j=3),
-                        in_=y[:].rearrange("p h j c -> p h (j c)"),
-                    )
-            else:
-                nc.sync.dma_start(
-                    out=out_t[b, 4 * s : 4 * s + 4, N1:512, :].rearrange("h p c -> p h c"),
-                    in_=y[:],
+                t = biased_pool.tile([P, WIDE], F32, name="biased")
+                col = 4 * sl + hh
+                nc.scalar.activation(
+                    out=t[:], in_=bank[:], func=IDENTITY, bias=bias_cols[:, col : col + 1],
+                    scale=projections[sl // 2][3],
                 )
+                biased[r].append(t)
 
-        w_regroup(0, 0, "v")
-        w_regroup(0, 1, "v")
-        w_quantise(0)
-        xg0 = x_transposes(0, "ssss")
-        x_quantise(0, xg0)
-        pb = ps2p.tile([P, 512], F32, name="ps2", tag="ps2")
-        nc.tensor.transpose(pb[:, 0:P], bt32[:], ident[:])
-        nc.scalar.mul(out=bcol[:, 0:16], in_=pb[:, 0:16], mul=Q_SCALE)
-        nc.scalar.copy(out=bcol[:, 16:32], in_=pb[:, 16:32])
-        xg1 = x_transposes(1, "ssvv")
+        back = {}
+
+        def transpose_back(r):
+            back[r] = []
+            for tl in range(4):
+                bank = back_banks.tile([P, WIDE], F32, name="back_bank")
+                for hh in range(4):
+                    nc.tensor.transpose(bank[:, P * hh : P * hh + P], biased[r][hh][:, P * tl : P * tl + P], ident[:])
+                back[r].append(bank)
+
+        y1_open = {}
+
+        def rope(r):
+            sl, grp = rounds[r]
+            heads = projections[sl // 2][2][:, 4 * (sl % 2) : 4 * (sl % 2) + 4, :, :]
+            for tl in range(4):
+                tile_no = 4 * grp + tl
+                slot = tile_no % 3 if grp < 3 else 3
+                bank = back[r][tl]
+                by_cos = products_pool.tile([P, 4, P], F32, name="by_cos")
+                nc.vector.tensor_tensor(
+                    out=by_cos[:],
+                    in0=bank[:].rearrange("p (h c) -> p h c", h=4),
+                    in1=cos_tab[:, slot, :].unsqueeze(1).to_broadcast([P, 4, P]),
+                    op=MULT,
+                )
+                by_sin = products_pool.tile([P, 4, P], F32, name="by_sin")
+                nc.vector.tensor_tensor(
+                    out=by_sin[:].rearrange("p h (j e) -> p h j e", e=2),
+                    in0=bank[:].rearrange("p (h j e) -> p h j e", h=4, e=2)[:, :, :, ::-1],
+                    in1=sin_pairs[:, slot, :, :].unsqueeze(1).to_broadcast([P, 4, P // 2, 2]),
+                    op=MULT,
+                )
+                if grp < 3:
+                    b, j = tile_no // 3, tile_no % 3
+                    if j == 0:
+                        y1_open[b] = y1_pool.tile([P, 4, 3, P], F32, name="y1")
+                    y = y1_open[b]
+                    nc.gpsimd.tensor_tensor(out=y[:, :, j, :], in0=by_cos[:], in1=by_sin[:], op=ADD)
+                    if j == 2:
+                        nc.sync.dma_start(
+                            out=heads[b, :, 0:N1, :].rearrange("h (p j) c -> p h (j c)", j=3),
+                            in_=y[:].rearrange("p h j c -> p h (j c)"),
+                        )
+                else:
+                    y = y2_pool.tile([P, 4, P], F32, name="y2")
+                    nc.gpsimd.tensor_tensor(out=y[:], in0=by_cos[:], in1=by_sin[:], op=ADD)
+                    nc.sync.dma_start(out=heads[tl, :, N1:WIDE, :].rearrange("h p c -> p h c"), in_=y[:])
+
+        for g in range(PASSES):
+            regroup_w(0, g, nc.vector.tensor_copy)
+        quantise_w(0)
+        transpose_x(0, nc.scalar.copy)
+        quantise_x(0)
+        bias_bank = back_banks.tile([P, WIDE], F32, name="back_bank")
+        nc.tensor.transpose(bias_bank[:, 0:P], bias_f32[:], ident[:])
+        for w in range(4):
+            nc.scalar.mul(
+                out=bias_cols[:, 8 * w : 8 * w + 8], in_=bias_bank[:, 8 * w : 8 * w + 8], mul=projections[w][3]
+            )
+        transpose_x(1, nc.vector.tensor_copy)
         project(0)
-        x_quantise(1, xg1)
+        quantise_x(1)
 
-        jobs = [(sl, g) for sl in range(1, 8) for g in range(2)]
-        quantise_after = {1: 1, 4: 2, 6: 3, 8: 4, 10: 5, 12: 6, 13: 7}
-        xg_late = {}
         for i in range(n_rounds):
-            back_transposes(i)
-            if i == 0:
-                xg_late[0] = (2, x_transposes(2, "ssss"))
+            transpose_back(i)
+            if i < 14:
+                regroup_w(1 + i // 2, i % 2, nc.scalar.copy)
+            if i < 2:
+                transpose_x(2 + i, nc.scalar.copy)
             if i + 1 < n_rounds:
                 project(i + 1)
-            if i == 4:
-                cast_tables(3, 4)
-            if i == 6:
-                xg_late[7] = (3, x_transposes(3, "ssss"))
-            if i < len(jobs):
-                w_regroup(jobs[i][0], jobs[i][1], "s")
-            for tl in range(4):
-                rope(i, tl)
-            if i in xg_late:
-                x_quantise(xg_late[i][0], xg_late[i][1])
-            if i in quantise_after:
-                w_quantise(quantise_after[i])
+            rope(i)
+            if i < 2:
+                quantise_x(2 + i)
+            if i < 14 and i % 2 == 1:
+                quantise_w(1 + i // 2)

from contextlib import ExitStack

import concourse.masks as masks
import concourse.mybir as mybir

F32 = mybir.dt.float32
BF16 = mybir.dt.bfloat16
U32 = mybir.dt.uint32
U8 = mybir.dt.uint8
FP8X4 = mybir.dt.float8_e4m3fn_x4
MULT = mybir.AluOpType.mult
ADD = mybir.AluOpType.add
IDENTITY = mybir.ActivationFunctionType.Identity

P = 128
D = 1024
PASSES = 2
WIDE = 512
N1 = 384
Q_SCALE = P ** -0.5
FLOPS = 2 * 2048 * 1024 * 2048


def tile_dualmultiheadattention_pa_kernel(
    tc, x_1, x_2, cos1, sin1, cos2, sin2, wq1, bq1, wk1, bk1, wq2, bq2, wk2, bk2, out_0, out_1
):
    nc = tc.nc
    projections = [
        (wq1, bq1, out_0, Q_SCALE, (0, 1, 2)),
        (wk1, bk1, out_1, 1.0, (0, 1, 2)),
        (wq2, bq2, out_0, Q_SCALE, (3,)),
        (wk2, bk2, out_1, 1.0, (3,)),
    ]
    rounds = [(sl, grp) for sl in range(8) for grp in projections[sl // 2][4]]
    n_rounds = len(rounds)

    with ExitStack() as ctx:
        const = ctx.enter_context(tc.tile_pool(name="const", bufs=1))
        raw = ctx.enter_context(tc.tile_pool(name="raw", bufs=1))
        x_grouped_pool = ctx.enter_context(tc.tile_pool(name="x_grouped", bufs=2))
        w_grouped_pool = ctx.enter_context(tc.tile_pool(name="w_grouped", bufs=2))
        w_codes_pool = ctx.enter_context(tc.tile_pool(name="w_codes", bufs=4))
        biased_pool = ctx.enter_context(tc.tile_pool(name="biased", bufs=8))
        products_pool = ctx.enter_context(tc.tile_pool(name="products", bufs=3))
        y1_pool = ctx.enter_context(tc.tile_pool(name="y1", bufs=3))
        y2_pool = ctx.enter_context(tc.tile_pool(name="y2", bufs=3))
        mx_banks = ctx.enter_context(tc.psum_pool(name="mx_banks", bufs=3))
        back_banks = ctx.enter_context(tc.psum_pool(name="back_banks", bufs=5))
        ctx.enter_context(tc.manual_schedule())

        ident = const.tile([P, P], F32, name="ident")
        masks.make_identity(nc, ident[:])

        bias_rows = const.tile([P, P], BF16, name="bias_rows")
        nc.vector.memset(bias_rows[:], 0.0)
        for w in range(4):
            nc.scalar.dma_start(
                out=bias_rows[8 * w : 8 * w + 8, :], in_=projections[w][1].rearrange("(h c) -> h c", c=P)
            )
        cos_bf = const.tile([P, 4, P], BF16, name="cos_bf")
        sin_bf = const.tile([P, 4, P], BF16, name="sin_bf")
        nc.scalar.dma_start(out=cos_bf[:, 0:3, :], in_=cos1.rearrange("(p j) c -> p j c", j=3))
        nc.scalar.dma_start(out=sin_bf[:, 0:3, :], in_=sin1.rearrange("(p j) c -> p j c", j=3))
        nc.scalar.dma_start(out=cos_bf[:, 3, :], in_=cos2)
        nc.scalar.dma_start(out=sin_bf[:, 3, :], in_=sin2)

        w_raw = [raw.tile([P, PASSES, 4, WIDE], BF16, name="w_raw%d" % sl) for sl in range(8)]

        def load_slice(sl):
            rows = projections[sl // 2][0].rearrange("(m q e) c -> q m e c", m=2 * PASSES, e=2)
            dst = w_raw[sl][:].rearrange("q g (u e) c -> q (g u) e c", e=2)
            first = WIDE * (sl % 2)
            for e in range(2):
                nc.sync.dma_start(out=dst[:, :, e, :], in_=rows[:, :, e, first : first + WIDE])

        x1_raw = [raw.tile([P, 3, D], BF16, name="x1_raw%d" % b) for b in range(4)]
        x2_raw = raw.tile([P, 4, D], BF16, name="x2_raw")
        load_slice(0)
        for b in range(4):
            nc.sync.dma_start(out=x1_raw[b][:], in_=x_1[b].rearrange("(p j) k -> p j k", j=3))
        load_slice(1)
        nc.sync.dma_start(out=x2_raw[:], in_=x_2.rearrange("b p k -> p b k"))
        for sl in range(2, 8):
            load_slice(sl)

        bias_f32 = const.tile([P, P], F32, name="bias_f32")
        nc.gpsimd.tensor_copy(out=bias_f32[:], in_=bias_rows[:])
        cos_tab = const.tile([P, 4, P], F32, name="cos_tab")
        nc.gpsimd.tensor_copy(out=cos_tab[:], in_=cos_bf[:])
        sin_tab = const.tile([P, 4, P], F32, name="sin_tab")
        sin_bf_pairs = sin_bf[:].rearrange("p s (j e) -> p s j e", e=2)
        sin_pairs = sin_tab[:].rearrange("p s (j e) -> p s j e", e=2)
        nc.gpsimd.tensor_scalar(
            out=sin_pairs[:, :, :, 0], in0=sin_bf_pairs[:, :, :, 0], scalar1=-1.0, scalar2=0.0, op0=MULT, op1=ADD
        )
        nc.gpsimd.tensor_copy(out=sin_pairs[:, :, :, 1], in_=sin_bf_pairs[:, :, :, 1])

        x_codes = [const.tile([P, PASSES, WIDE], U32, name="x_codes%d" % g, align_bytes=64) for g in range(4)]
        x_scales = [const.tile([P, PASSES, WIDE], U8, name="x_scales%d" % g, align_bytes=64) for g in range(4)]
        x_grouped = {}

        def transpose_x(grp, copy):
            x_grouped[grp] = x_grouped_pool.tile([P, PASSES, WIDE, 4], BF16, name="x_grouped", align_bytes=64)
            words = x_grouped[grp][:].bitcast(F32)
            for tl in range(4):
                tile_no = 4 * grp + tl
                if grp < 3:
                    tokens = x1_raw[tile_no // 3][:, tile_no % 3, :].bitcast(F32)
                else:
                    tokens = x2_raw[:, tl, :].bitcast(F32)
                bank = mx_banks.tile([P, WIDE], F32, name="mx_bank")
                for m in range(2 * PASSES):
                    nc.tensor.transpose(bank[:, P * m : P * m + P], tokens[:, P * m : P * m + P], ident[:])
                copy(
                    out=words[:, :, P * tl : P * tl + P, :],
                    in_=bank[:].rearrange("p (g u t) -> p g t u", g=PASSES, u=2),
                )

        def quantise_x(grp):
            nc.vector.quantize_mx(
                out=x_codes[grp][:].rearrange("p g t -> p (g t)").bitcast(FP8X4),
                scales=x_scales[grp][:].rearrange("p g t -> p (g t)"),
                in_=x_grouped[grp][:].rearrange("p g t k -> p (g t k)"),
            )

        w_grouped = {}
        w_codes = {}

        def regroup_w(sl, g, copy):
            if g == 0:
                w_grouped[sl] = w_grouped_pool.tile([P, PASSES, WIDE, 4], BF16, name="w_grouped", align_bytes=64)
            copy(
                out=w_grouped[sl][:, g, :, :].rearrange("p (c i) t -> p c t i", i=4),
                in_=w_raw[sl][:, g, :, :].rearrange("p t (c i) -> p c t i", i=4),
            )

        def quantise_w(sl):
            codes = w_codes_pool.tile([P, PASSES, WIDE], U32, name="w_code_words", align_bytes=64)
            scales = w_codes_pool.tile([P, PASSES, WIDE], U8, name="w_scales", align_bytes=64)
            nc.vector.quantize_mx(
                out=codes[:].rearrange("p g c -> p (g c)").bitcast(FP8X4),
                scales=scales[:].rearrange("p g c -> p (g c)"),
                in_=w_grouped[sl][:].rearrange("p g c t -> p (g c t)"),
            )
            w_codes[sl] = (codes, scales)

        bias_cols = const.tile([P, 32], F32, name="bias_cols")
        biased = {}

        def project(r):
            sl, grp = rounds[r]
            codes, scales = w_codes[sl]
            biased[r] = []
            for hh in range(4):
                bank = mx_banks.tile([P, WIDE], F32, name="mx_bank")
                for g in range(PASSES):
                    nc.tensor.matmul_mx(
                        out=bank[:],
                        lhsT=codes[:, g, P * hh : P * hh + P].bitcast(FP8X4),
                        lhsT_scale=scales[:, g, P * hh : P * hh + P],
                        rhs=x_codes[grp][:, g, :].bitcast(FP8X4),
                        rhs_scale=x_scales[grp][:, g, :],
                        start=(g == 0),
                        stop=(g == PASSES - 1),
                    )
                t = biased_pool.tile([P, WIDE], F32, name="biased")
                col = 4 * sl + hh
                nc.scalar.activation(
                    out=t[:], in_=bank[:], func=IDENTITY, bias=bias_cols[:, col : col + 1],
                    scale=projections[sl // 2][3],
                )
                biased[r].append(t)

        back = {}

        def transpose_back(r):
            back[r] = []
            for tl in range(4):
                bank = back_banks.tile([P, WIDE], F32, name="back_bank")
                for hh in range(4):
                    nc.tensor.transpose(bank[:, P * hh : P * hh + P], biased[r][hh][:, P * tl : P * tl + P], ident[:])
                back[r].append(bank)

        y1_open = {}

        def rope(r):
            sl, grp = rounds[r]
            heads = projections[sl // 2][2][:, 4 * (sl % 2) : 4 * (sl % 2) + 4, :, :]
            for tl in range(4):
                tile_no = 4 * grp + tl
                slot = tile_no % 3 if grp < 3 else 3
                bank = back[r][tl]
                by_cos = products_pool.tile([P, 4, P], F32, name="by_cos")
                nc.vector.tensor_tensor(
                    out=by_cos[:],
                    in0=bank[:].rearrange("p (h c) -> p h c", h=4),
                    in1=cos_tab[:, slot, :].unsqueeze(1).to_broadcast([P, 4, P]),
                    op=MULT,
                )
                by_sin = products_pool.tile([P, 4, P], F32, name="by_sin")
                nc.vector.tensor_tensor(
                    out=by_sin[:].rearrange("p h (j e) -> p h j e", e=2),
                    in0=bank[:].rearrange("p (h j e) -> p h j e", h=4, e=2)[:, :, :, ::-1],
                    in1=sin_pairs[:, slot, :, :].unsqueeze(1).to_broadcast([P, 4, P // 2, 2]),
                    op=MULT,
                )
                if grp < 3:
                    b, j = tile_no // 3, tile_no % 3
                    if j == 0:
                        y1_open[b] = y1_pool.tile([P, 4, 3, P], F32, name="y1")
                    y = y1_open[b]
                    nc.gpsimd.tensor_tensor(out=y[:, :, j, :], in0=by_cos[:], in1=by_sin[:], op=ADD)
                    if j == 2:
                        nc.sync.dma_start(
                            out=heads[b, :, 0:N1, :].rearrange("h (p j) c -> p h (j c)", j=3),
                            in_=y[:].rearrange("p h j c -> p h (j c)"),
                        )
                else:
                    y = y2_pool.tile([P, 4, P], F32, name="y2")
                    nc.gpsimd.tensor_tensor(out=y[:], in0=by_cos[:], in1=by_sin[:], op=ADD)
                    nc.sync.dma_start(out=heads[tl, :, N1:WIDE, :].rearrange("h p c -> p h c"), in_=y[:])

        for g in range(PASSES):
            regroup_w(0, g, nc.vector.tensor_copy)
        quantise_w(0)
        transpose_x(0, nc.scalar.copy)
        quantise_x(0)
        bias_bank = back_banks.tile([P, WIDE], F32, name="back_bank")
        nc.tensor.transpose(bias_bank[:, 0:P], bias_f32[:], ident[:])
        for w in range(4):
            nc.scalar.mul(
                out=bias_cols[:, 8 * w : 8 * w + 8], in_=bias_bank[:, 8 * w : 8 * w + 8], mul=projections[w][3]
            )
        transpose_x(1, nc.vector.tensor_copy)
        project(0)
        quantise_x(1)

        for i in range(n_rounds):
            transpose_back(i)
            if i < 14:
                regroup_w(1 + i // 2, i % 2, nc.scalar.copy)
            if i < 2:
                transpose_x(2 + i, nc.scalar.copy)
            if i + 1 < n_rounds:
                project(i + 1)
            rope(i)
            if i < 2:
                quantise_x(2 + i)
            if i < 14 and i % 2 == 1:
                quantise_w(1 + i // 2)
